import numpy as np
import ml_dtypes


def mxq(x, axis, fmt="e4m3"):
    dtype, down = {"e4m3": (ml_dtypes.float8_e4m3fn, 7), "e5m2": (ml_dtypes.float8_e5m2, 14)}[fmt]
    v = np.moveaxis(np.asarray(x, np.float32).astype(ml_dtypes.bfloat16).astype(np.float64), axis, -1)
    blocks = v.reshape(v.shape[:-1] + (-1, 32))
    amax = np.abs(blocks).max(-1, keepdims=True)
    byte = np.maximum(np.where(amax > 0, np.frexp(amax)[1] - 1 + 127, 0) - down, 1)
    scale = np.exp2(byte - 127.0)
    codes = (blocks / scale).astype(np.float32).astype(dtype).astype(np.float64)
    return np.moveaxis((codes * scale).reshape(v.shape), -1, axis)


WIDE = False


def mx_kscale(k):
    if not WIDE:
        return np.ones(k)
    levels = np.array([10, -10, 5, -5, 0])
    a = np.random.permutation(np.resize(levels, k // 512 * 4)).reshape(k // 512, 4)
    idx = np.arange(k)
    return np.exp2(a[idx // 512, idx % 128 // 32])


BF16 = ml_dtypes.bfloat16


def bf(x):
    return np.asarray(x, np.float32).astype(BF16)


def f64(x):
    return np.asarray(x).astype(np.float64)


N, IN_CH, OUT_CH = 1024, 512, 512
K2 = IN_CH + IN_CH
K3 = K2 + IN_CH


def setup_inputs():
    s = mx_kscale(K3)
    return {
        'q': bf(np.random.standard_normal((N, OUT_CH)) * 2.0),
        'k1': bf(np.random.standard_normal((N, OUT_CH)) * 2.0),
        'k2': bf(np.random.standard_normal((N, OUT_CH)) * 2.0),
        'sp': bf(np.random.standard_normal((N, IN_CH)) * s[:IN_CH]),
        'om1': bf(np.random.standard_normal((N, IN_CH)) * s[IN_CH:K2]),
        'om2': bf(np.random.standard_normal((N, IN_CH)) * s[K2:]),
        'v_w': bf(np.random.standard_normal((OUT_CH, K3)) * 2.0 / np.sqrt(K3) / s[None, :]),
        'v_b': bf(np.random.standard_normal(OUT_CH) * 0.3),
    }


def reference(q, k1, k2, sp, om1, om2, v_w, v_b):
    om_cat = np.concatenate([f64(sp), f64(om1), f64(om2)], axis=-1)
    v = (mxq(om_cat, 1, 'e4m3') @ mxq(f64(v_w), 1, 'e4m3').T) + f64(v_b)
    vq = mxq(v, 0, 'e4m3')
    scale = 1.0 / np.sqrt(OUT_CH)
    s1 = f64(q) @ f64(k1).T * scale
    s2 = f64(q) @ f64(k2).T * scale
    e1 = np.exp(s1 - s1.max(-1, keepdims=True))
    e2 = np.exp(s2 - s2.max(-1, keepdims=True))
    attn1 = (mxq(e1, 1, 'e4m3') @ vq) / e1.sum(-1, keepdims=True)
    attn2 = (mxq(e2, 1, 'e4m3') @ vq) / e2.sum(-1, keepdims=True)
    return attn1, attn2

@@ -1,0 +1,209 @@
+from contextlib import ExitStack
+import math
+
+import concourse.mybir as mybir
+from concourse.masks import make_identity
+
+F32 = mybir.dt.float32
+BF16 = mybir.dt.bfloat16
+U32 = mybir.dt.uint32
+U8 = mybir.dt.uint8
+FP8X4 = mybir.dt.float8_e4m3fn_x4
+ACT = mybir.ActivationFunctionType
+ALU = mybir.AluOpType
+AXIS = mybir.AxisListType
+
+P = 128
+TOKENS = 1024
+WIDTH = 512
+STREAMS = 3
+ROW_TILES = TOKENS // P
+KEY_PASSES = TOKENS // 512
+SCORE_SCALE = 1.0 / math.sqrt(WIDTH)
+
+FLOPS = 2 * TOKENS * STREAMS * WIDTH * WIDTH + 4 * 2 * TOKENS * TOKENS * WIDTH
+
+
+def tile_sc_attn_pa_kernel(tc, q, k1, k2, sp, om1, om2, v_w, v_b, out_0, out_1):
+    nc = tc.nc
+    with ExitStack() as ctx:
+        const = ctx.enter_context(tc.tile_pool(name="const", bufs=1))
+        inputs = ctx.enter_context(tc.tile_pool(name="inputs", bufs=1))
+        keep = ctx.enter_context(tc.tile_pool(name="keep", bufs=1))
+        stage = ctx.enter_context(tc.tile_pool(name="stage", bufs=4))
+        soft = ctx.enter_context(tc.tile_pool(name="soft", bufs=3))
+        psum = ctx.enter_context(tc.psum_pool(name="psum", bufs=8))
+
+        def load_key_rows(x, name):
+            rows = inputs.tile([P, ROW_TILES, WIDTH], BF16, name=name)
+            view = x.rearrange("(g p t) c -> p g t c", g=KEY_PASSES, p=P, t=4)
+            for g in range(KEY_PASSES):
+                nc.sync.dma_start(out=rows[:, 4 * g : 4 * g + 4, :], in_=view[:, g])
+            return rows
+
+        bias_rows = const.tile([P, WIDTH], BF16)
+        nc.gpsimd.dma_start(out=bias_rows[:], in_=v_b.partition_broadcast(P))
+        ident_words = const.tile([P, P], F32)
+        make_identity(nc, ident_words[:])
+        ident_bf16 = const.tile([P, P], BF16)
+        make_identity(nc, ident_bf16[:])
+
+        k_rows = [load_key_rows(k1, "k1_rows")]
+        q_rows = inputs.tile([P, ROW_TILES, WIDTH], BF16)
+        q_view = q.rearrange("(p t) c -> p t c", t=ROW_TILES)
+        for half in range(2):
+            nc.sync.dma_start(out=q_rows[:, 4 * half : 4 * half + 4, :], in_=q_view[:, 4 * half : 4 * half + 4, :])
+        w_rows = inputs.tile([P, WIDTH // P, STREAMS * WIDTH], BF16)
+        w_view = v_w.rearrange("(t p) f -> p t f", p=P)
+        for half in range(2):
+            nc.sync.dma_start(out=w_rows[:, 2 * half : 2 * half + 2, :], in_=w_view[:, 2 * half : 2 * half + 2, :])
+        stream_rows = [load_key_rows(sp, "sp_rows"), load_key_rows(om1, "om1_rows"), load_key_rows(om2, "om2_rows")]
+        k_rows.append(load_key_rows(k2, "k2_rows"))
+
+        def flip_two_row_tiles(words, first_tile):
+            bank = psum.tile([P, 2, 2, P], F32, tag="bank")
+            for k in range(2):
+                for u in range(2):
+                    nc.tensor.transpose(bank[:, k, u, :], words[:, first_tile + k, u * P : (u + 1) * P], ident_words[:])
+            return bank
+
+        def copy_out(bank_number, out, in_):
+            if bank_number % 2 == 0:
+                nc.vector.tensor_copy(out=out, in_=in_)
+            else:
+                nc.scalar.copy(out=out, in_=in_)
+
+        def flip_for_scores(rows, name):
+            flipped = keep.tile([P, 2, 2 * TOKENS], BF16, name=name)
+            flipped_words = flipped[:].bitcast(F32)
+            words = rows[:].bitcast(F32)
+            for pair in range(ROW_TILES // 2):
+                bank = flip_two_row_tiles(words, 2 * pair)
+                copy_out(
+                    pair,
+                    flipped_words[:, :, 2 * P * pair : 2 * P * (pair + 1)].rearrange("p u (k r) -> p u k r", k=2),
+                    bank[:].rearrange("p k u r -> p u k r"),
+                )
+            return flipped[:].rearrange("p u (r e) -> p u r e", e=2)
+
+        def flip_and_quantise(words, row_tiles, codes, scales):
+            for pair in range(row_tiles // 2):
+                bank = flip_two_row_tiles(words, 2 * pair)
+                grouped = stage.tile([P, 8 * P], BF16, align_bytes=64)
+                copy_out(
+                    pair,
+                    grouped[:].bitcast(F32).rearrange("p (k r u) -> p k r u", k=2, u=2),
+                    bank[:].rearrange("p k u r -> p k r u"),
+                )
+                cols = slice(2 * P * pair, 2 * P * (pair + 1))
+                nc.vector.quantize_mx(out=codes[:, cols].bitcast(FP8X4), scales=scales[:, cols], in_=grouped[:])
+
+        kT = [flip_for_scores(k_rows[0], "k1T")]
+        qT = flip_for_scores(q_rows, "qT")
+
+        w_codes = keep.tile([P, STREAMS, WIDTH], U32, align_bytes=64)
+        w_scales = keep.tile([P, STREAMS, WIDTH], U8, align_bytes=64)
+        om_codes = keep.tile([P, STREAMS, TOKENS], U32, align_bytes=64)
+        om_scales = keep.tile([P, STREAMS, TOKENS], U8, align_bytes=64)
+        w_words = w_rows[:].bitcast(F32)
+        for s in range(STREAMS):
+            flip_and_quantise(
+                w_words[:, :, (WIDTH // 2) * s : (WIDTH // 2) * (s + 1)], WIDTH // P, w_codes[:, s, :], w_scales[:, s, :]
+            )
+        for s in range(STREAMS):
+            flip_and_quantise(stream_rows[s][:].bitcast(F32), ROW_TILES, om_codes[:, s, :], om_scales[:, s, :])
+
+        v_rows = keep.tile([P, ROW_TILES, WIDTH], BF16)
+        for kt in range(ROW_TILES):
+            keys = slice(kt * P, (kt + 1) * P)
+            v_bank = psum.tile([P, WIDTH], F32, tag="bank")
+            for s in range(STREAMS):
+                nc.tensor.matmul_mx(
+                    out=v_bank[:],
+                    lhsT=om_codes[:, s, keys].bitcast(FP8X4),
+                    lhsT_scale=om_scales[:, s, keys],
+                    rhs=w_codes[:, s, :].bitcast(FP8X4),
+                    rhs_scale=w_scales[:, s, :],
+                    start=(s == 0),
+                    stop=(s == STREAMS - 1),
+                )
+            nc.vector.tensor_tensor(out=v_rows[:, kt, :], in0=v_bank[:], in1=bias_rows[:], op=ALU.add)
+
+        v_grouped = keep.tile([P, KEY_PASSES, WIDTH, 4], BF16, align_bytes=64)
+        v_codes = keep.tile([P, KEY_PASSES, WIDTH], U32, align_bytes=64)
+        v_scales = keep.tile([P, KEY_PASSES, WIDTH], U8, align_bytes=64)
+        for g in range(KEY_PASSES):
+            nc.vector.tensor_copy(out=v_grouped[:, g], in_=v_rows[:, 4 * g : 4 * g + 4, :].rearrange("p t c -> p c t"))
+        for g in range(KEY_PASSES):
+            nc.vector.quantize_mx(
+                out=v_codes[:, g, :].bitcast(FP8X4),
+                scales=v_scales[:, g, :],
+                in_=v_grouped[:, g].rearrange("p c t -> p (c t)"),
+            )
+
+        kT.append(flip_for_scores(k_rows[1], "k2T"))
+
+        out_views = [o.rearrange("(p t) c -> p t c", t=ROW_TILES) for o in (out_0, out_1)]
+        for j in range(2):
+            for qt in range(ROW_TILES):
+                queries = slice(qt * P, (qt + 1) * P)
+                s_banks = []
+                row_max = soft.tile([P, 2], F32)
+                for h in range(2):
+                    s_bank = psum.tile([P, 512], F32, tag="bank")
+                    for u in range(2):
+                        for e in range(2):
+                            nc.tensor.matmul(
+                                out=s_bank[:],
+                                lhsT=qT[:, u, queries, e],
+                                rhs=kT[j][:, u, 512 * h : 512 * (h + 1), e],
+                                start=(u == 0 and e == 0),
+                                stop=(u == 1 and e == 1),
+                            )
+                    nc.vector.reduce_max(out=row_max[:, h : h + 1], in_=s_bank[:], axis=AXIS.X)
+                    s_banks.append(s_bank)
+                neg_max = soft.tile([P, 1], F32)
+                nc.vector.tensor_scalar(
+                    out=neg_max[:], in0=row_max[:, 0:1], scalar1=row_max[:, 1:2], scalar2=-SCORE_SCALE,
+                    op0=ALU.max, op1=ALU.mult,
+                )
+                e_rows = soft.tile([P, ROW_TILES, P], BF16)
+                half_sums = soft.tile([P, 2], F32)
+                for h in range(2):
+                    nc.scalar.activation(
+                        out=e_rows[:, 4 * h : 4 * h + 4, :].rearrange("p t r -> p (t r)"),
+                        in_=s_banks[h][:],
+                        func=ACT.Exp,
+                        bias=neg_max[:, 0:1],
+                        scale=SCORE_SCALE,
+                        accum_out=half_sums[:, h : h + 1],
+                    )
+                row_scale = soft.tile([P, 1], F32)
+                nc.vector.reduce_sum(out=row_scale[:], in_=half_sums[:], axis=AXIS.X)
+                nc.vector.reciprocal(out=row_scale[:], in_=row_scale[:])
+                e_bank = psum.tile([P, ROW_TILES, P], BF16, tag="bank")
+                for kt in range(ROW_TILES):
+                    nc.tensor.transpose(e_bank[:, kt, :], e_rows[:, kt, :], ident_bf16[:])
+                e_grouped = soft.tile([P, KEY_PASSES, P, 4], BF16, align_bytes=64)
+                nc.scalar.copy(out=e_grouped[:], in_=e_bank[:].rearrange("p (g t) r -> p g r t", g=KEY_PASSES))
+                e_codes = soft.tile([P, KEY_PASSES, P], U32, align_bytes=64)
+                e_scales = soft.tile([P, KEY_PASSES, P], U8, align_bytes=64)
+                nc.vector.quantize_mx(
+                    out=e_codes[:].rearrange("p g r -> p (g r)").bitcast(FP8X4),
+                    scales=e_scales[:].rearrange("p g r -> p (g r)"),
+                    in_=e_grouped[:].rearrange("p g r t -> p (g r t)"),
+                )
+                o_bank = psum.tile([P, WIDTH], F32, tag="bank")
+                for g in range(KEY_PASSES):
+                    nc.tensor.matmul_mx(
+                        out=o_bank[:],
+                        lhsT=e_codes[:, g, :].bitcast(FP8X4),
+                        lhsT_scale=e_scales[:, g, :],
+                        rhs=v_codes[:, g, :].bitcast(FP8X4),
+                        rhs_scale=v_scales[:, g, :],
+                        start=(g == 0),
+                        stop=(g == KEY_PASSES - 1),
+                    )
+                o_rows = stage.tile([P, WIDTH], F32)
+                nc.vector.tensor_scalar(out=o_rows[:], in0=o_bank[:], scalar1=row_scale[:, 0:1], scalar2=None, op0=ALU.mult)
+                nc.sync.dma_start(out=out_views[j][:, qt, :], in_=o_rows[:])

@@ -14,11 +14,13 @@ ALU = mybir.AluOpType
 AXIS = mybir.AxisListType
 
 P = 128
+PACK = 4
 TOKENS = 1024
 WIDTH = 512
 STREAMS = 3
 ROW_TILES = TOKENS // P
-KEY_PASSES = TOKENS // 512
+KEY_PASSES = TOKENS // (P * PACK)
+ROUNDS = 2 * ROW_TILES
 SCORE_SCALE = 1.0 / math.sqrt(WIDTH)
 
 FLOPS = 2 * TOKENS * STREAMS * WIDTH * WIDTH + 4 * 2 * TOKENS * TOKENS * WIDTH
@@ -27,183 +29,271 @@ FLOPS = 2 * TOKENS * STREAMS * WIDTH * WIDTH + 4 * 2 * TOKENS * TOKENS * WIDTH
 def tile_sc_attn_pa_kernel(tc, q, k1, k2, sp, om1, om2, v_w, v_b, out_0, out_1):
     nc = tc.nc
     with ExitStack() as ctx:
+        ctx.enter_context(tc.manual_schedule())
         const = ctx.enter_context(tc.tile_pool(name="const", bufs=1))
         inputs = ctx.enter_context(tc.tile_pool(name="inputs", bufs=1))
         keep = ctx.enter_context(tc.tile_pool(name="keep", bufs=1))
         stage = ctx.enter_context(tc.tile_pool(name="stage", bufs=4))
         soft = ctx.enter_context(tc.tile_pool(name="soft", bufs=3))
+        stats = ctx.enter_context(tc.tile_pool(name="stats", bufs=6))
         psum = ctx.enter_context(tc.psum_pool(name="psum", bufs=8))
 
-        def load_key_rows(x, name):
-            rows = inputs.tile([P, ROW_TILES, WIDTH], BF16, name=name)
-            view = x.rearrange("(g p t) c -> p g t c", g=KEY_PASSES, p=P, t=4)
-            for g in range(KEY_PASSES):
-                nc.sync.dma_start(out=rows[:, 4 * g : 4 * g + 4, :], in_=view[:, g])
-            return rows
-
-        bias_rows = const.tile([P, WIDTH], BF16)
-        nc.gpsimd.dma_start(out=bias_rows[:], in_=v_b.partition_broadcast(P))
         ident_words = const.tile([P, P], F32)
         make_identity(nc, ident_words[:])
         ident_bf16 = const.tile([P, P], BF16)
         make_identity(nc, ident_bf16[:])
+        bias_rows = const.tile([P, WIDTH], BF16)
+        nc.gpsimd.dma_start(out=bias_rows[:], in_=v_b.partition_broadcast(P))
 
-        k_rows = [load_key_rows(k1, "k1_rows")]
+        w_rows = inputs.tile([P, WIDTH // P, STREAMS * WIDTH], BF16)
+        w_view = v_w.rearrange("(t p) f -> p t f", p=P)
+        for s in range(STREAMS):
+            features = slice(s * WIDTH, (s + 1) * WIDTH)
+            nc.sync.dma_start(out=w_rows[:, :, features], in_=w_view[:, :, features])
+
+        def load_key_rows(rows, x, g):
+            view = x.rearrange("(g p t) c -> p g t c", g=KEY_PASSES, p=P, t=PACK)
+            nc.sync.dma_start(out=rows[:, PACK * g : PACK * (g + 1), :], in_=view[:, g])
+
+        stream_rows = [inputs.tile([P, ROW_TILES, WIDTH], BF16, name="stream_rows%d" % s) for s in range(STREAMS)]
+        for g in range(KEY_PASSES):
+            for s, x in enumerate((sp, om1, om2)):
+                load_key_rows(stream_rows[s], x, g)
+        k_rows = [inputs.tile([P, ROW_TILES, WIDTH], BF16, name="k_rows%d" % j) for j in range(2)]
+        for g in range(KEY_PASSES):
+            load_key_rows(k_rows[0], k1, g)
         q_rows = inputs.tile([P, ROW_TILES, WIDTH], BF16)
         q_view = q.rearrange("(p t) c -> p t c", t=ROW_TILES)
         for half in range(2):
-            nc.sync.dma_start(out=q_rows[:, 4 * half : 4 * half + 4, :], in_=q_view[:, 4 * half : 4 * half + 4, :])
-        w_rows = inputs.tile([P, WIDTH // P, STREAMS * WIDTH], BF16)
-        w_view = v_w.rearrange("(t p) f -> p t f", p=P)
-        for half in range(2):
-            nc.sync.dma_start(out=w_rows[:, 2 * half : 2 * half + 2, :], in_=w_view[:, 2 * half : 2 * half + 2, :])
-        stream_rows = [load_key_rows(sp, "sp_rows"), load_key_rows(om1, "om1_rows"), load_key_rows(om2, "om2_rows")]
-        k_rows.append(load_key_rows(k2, "k2_rows"))
+            tiles = slice(half * ROW_TILES // 2, (half + 1) * ROW_TILES // 2)
+            nc.sync.dma_start(out=q_rows[:, tiles, :], in_=q_view[:, tiles, :])
+        for g in range(KEY_PASSES):
+            load_key_rows(k_rows[1], k2, g)
 
-        def flip_two_row_tiles(words, first_tile):
+        def word_transposes(words, pair):
             bank = psum.tile([P, 2, 2, P], F32, tag="bank")
-            for k in range(2):
-                for u in range(2):
-                    nc.tensor.transpose(bank[:, k, u, :], words[:, first_tile + k, u * P : (u + 1) * P], ident_words[:])
-            return bank
+            jobs = [
+                (bank[:, k, u, :], words[:, 2 * pair + k, u * P : (u + 1) * P], ident_words[:])
+                for k in range(2)
+                for u in range(2)
+            ]
+            return bank, jobs
 
-        def copy_out(bank_number, out, in_):
-            if bank_number % 2 == 0:
-                nc.vector.tensor_copy(out=out, in_=in_)
-            else:
-                nc.scalar.copy(out=out, in_=in_)
+        def flip_and_quantise(words, pair, codes, scales):
+            bank, jobs = word_transposes(words, pair)
+            for job in jobs:
+                nc.tensor.transpose(*job)
+            grouped = stage.tile([P, 2 * P * PACK], BF16, align_bytes=64)
+            nc.scalar.copy(
+                out=grouped[:].bitcast(F32).rearrange("p (k r u) -> p k r u", k=2, u=2),
+                in_=bank[:].rearrange("p k u r -> p k r u"),
+            )
+            cols = slice(2 * P * pair, 2 * P * (pair + 1))
+            nc.vector.quantize_mx(out=codes[:, cols].bitcast(FP8X4), scales=scales[:, cols], in_=grouped[:])
 
-        def flip_for_scores(rows, name):
-            flipped = keep.tile([P, 2, 2 * TOKENS], BF16, name=name)
-            flipped_words = flipped[:].bitcast(F32)
-            words = rows[:].bitcast(F32)
-            for pair in range(ROW_TILES // 2):
-                bank = flip_two_row_tiles(words, 2 * pair)
-                copy_out(
-                    pair,
-                    flipped_words[:, :, 2 * P * pair : 2 * P * (pair + 1)].rearrange("p u (k r) -> p u k r", k=2),
-                    bank[:].rearrange("p k u r -> p u k r"),
-                )
-            return flipped[:].rearrange("p u (r e) -> p u r e", e=2)
-
-        def flip_and_quantise(words, row_tiles, codes, scales):
-            for pair in range(row_tiles // 2):
-                bank = flip_two_row_tiles(words, 2 * pair)
-                grouped = stage.tile([P, 8 * P], BF16, align_bytes=64)
-                copy_out(
-                    pair,
-                    grouped[:].bitcast(F32).rearrange("p (k r u) -> p k r u", k=2, u=2),
-                    bank[:].rearrange("p k u r -> p k r u"),
-                )
-                cols = slice(2 * P * pair, 2 * P * (pair + 1))
-                nc.vector.quantize_mx(out=codes[:, cols].bitcast(FP8X4), scales=scales[:, cols], in_=grouped[:])
-
-        kT = [flip_for_scores(k_rows[0], "k1T")]
-        qT = flip_for_scores(q_rows, "qT")
+        def score_operand_slot(flipped, pair):
+            rows = slice(2 * P * pair, 2 * P * (pair + 1))
+            return flipped[:].bitcast(F32)[:, :, rows].rearrange("p u (k r) -> p u k r", k=2)
 
         w_codes = keep.tile([P, STREAMS, WIDTH], U32, align_bytes=64)
         w_scales = keep.tile([P, STREAMS, WIDTH], U8, align_bytes=64)
         om_codes = keep.tile([P, STREAMS, TOKENS], U32, align_bytes=64)
         om_scales = keep.tile([P, STREAMS, TOKENS], U8, align_bytes=64)
-        w_words = w_rows[:].bitcast(F32)
-        for s in range(STREAMS):
-            flip_and_quantise(
-                w_words[:, :, (WIDTH // 2) * s : (WIDTH // 2) * (s + 1)], WIDTH // P, w_codes[:, s, :], w_scales[:, s, :]
-            )
-        for s in range(STREAMS):
-            flip_and_quantise(stream_rows[s][:].bitcast(F32), ROW_TILES, om_codes[:, s, :], om_scales[:, s, :])
-
         v_rows = keep.tile([P, ROW_TILES, WIDTH], BF16)
-        for kt in range(ROW_TILES):
-            keys = slice(kt * P, (kt + 1) * P)
-            v_bank = psum.tile([P, WIDTH], F32, tag="bank")
-            for s in range(STREAMS):
-                nc.tensor.matmul_mx(
-                    out=v_bank[:],
-                    lhsT=om_codes[:, s, keys].bitcast(FP8X4),
-                    lhsT_scale=om_scales[:, s, keys],
-                    rhs=w_codes[:, s, :].bitcast(FP8X4),
-                    rhs_scale=w_scales[:, s, :],
-                    start=(s == 0),
-                    stop=(s == STREAMS - 1),
-                )
-            nc.vector.tensor_tensor(out=v_rows[:, kt, :], in0=v_bank[:], in1=bias_rows[:], op=ALU.add)
-
-        v_grouped = keep.tile([P, KEY_PASSES, WIDTH, 4], BF16, align_bytes=64)
+        v_grouped = keep.tile([P, KEY_PASSES, WIDTH, PACK], BF16, align_bytes=64)
         v_codes = keep.tile([P, KEY_PASSES, WIDTH], U32, align_bytes=64)
         v_scales = keep.tile([P, KEY_PASSES, WIDTH], U8, align_bytes=64)
-        for g in range(KEY_PASSES):
-            nc.vector.tensor_copy(out=v_grouped[:, g], in_=v_rows[:, 4 * g : 4 * g + 4, :].rearrange("p t c -> p c t"))
-        for g in range(KEY_PASSES):
+
+        def project_keys(g):
+            for kt in range(PACK * g, PACK * (g + 1)):
+                keys = slice(kt * P, (kt + 1) * P)
+                v_bank = psum.tile([P, WIDTH], F32, tag="bank")
+                for s in range(STREAMS):
+                    nc.tensor.matmul_mx(
+                        out=v_bank[:],
+                        lhsT=om_codes[:, s, keys].bitcast(FP8X4),
+                        lhsT_scale=om_scales[:, s, keys],
+                        rhs=w_codes[:, s, :].bitcast(FP8X4),
+                        rhs_scale=w_scales[:, s, :],
+                        start=(s == 0),
+                        stop=(s == STREAMS - 1),
+                    )
+                nc.vector.tensor_tensor(out=v_rows[:, kt, :], in0=v_bank[:], in1=bias_rows[:], op=ALU.add)
+
+        def quantise_v(g):
+            nc.vector.tensor_copy(
+                out=v_grouped[:, g], in_=v_rows[:, PACK * g : PACK * (g + 1), :].rearrange("p t c -> p c t")
+            )
             nc.vector.quantize_mx(
                 out=v_codes[:, g, :].bitcast(FP8X4),
                 scales=v_scales[:, g, :],
                 in_=v_grouped[:, g].rearrange("p c t -> p (c t)"),
             )
 
-        kT.append(flip_for_scores(k_rows[1], "k2T"))
+        w_words = w_rows[:].bitcast(F32)
+        for s in range(STREAMS):
+            for pair in range(WIDTH // P // 2):
+                flip_and_quantise(
+                    w_words[:, :, (WIDTH // 2) * s : (WIDTH // 2) * (s + 1)], pair, w_codes[:, s, :], w_scales[:, s, :]
+                )
+        for g in range(KEY_PASSES):
+            for s in range(STREAMS):
+                for pair in range(2 * g, 2 * g + 2):
+                    flip_and_quantise(stream_rows[s][:].bitcast(F32), pair, om_codes[:, s, :], om_scales[:, s, :])
+            if g > 0:
+                quantise_v(g - 1)
+            project_keys(g)
 
+        qT = keep.tile([P, 2, 2 * TOKENS], BF16)
+        kT = [keep.tile([P, 2, 2 * TOKENS], BF16, name="kT%d" % j) for j in range(2)]
+        first_banks = [(k_rows[0], kT[0], pair) for pair in range(ROW_TILES // 2)] + [(q_rows, qT, 0)]
+        side_banks = [(q_rows, qT, pair) for pair in range(1, ROW_TILES // 2)]
+        side_banks += [(k_rows[1], kT[1], pair) for pair in range(ROW_TILES // 2)]
+        for rows, flipped, pair in first_banks:
+            bank, jobs = word_transposes(rows[:].bitcast(F32), pair)
+            for job in jobs:
+                nc.tensor.transpose(*job)
+            nc.scalar.copy(out=score_operand_slot(flipped, pair), in_=bank[:].rearrange("p k u r -> p u k r"))
+        quantise_v(KEY_PASSES - 1)
+
+        q_steps = qT[:].rearrange("p u (r e) -> p u r e", e=2)
+        k_steps = [kT[j][:].rearrange("p u (r e) -> p u r e", e=2) for j in range(2)]
         out_views = [o.rearrange("(p t) c -> p t c", t=ROW_TILES) for o in (out_0, out_1)]
-        for j in range(2):
-            for qt in range(ROW_TILES):
-                queries = slice(qt * P, (qt + 1) * P)
-                s_banks = []
-                row_max = soft.tile([P, 2], F32)
-                for h in range(2):
-                    s_bank = psum.tile([P, 512], F32, tag="bank")
-                    for u in range(2):
-                        for e in range(2):
-                            nc.tensor.matmul(
-                                out=s_bank[:],
-                                lhsT=qT[:, u, queries, e],
-                                rhs=kT[j][:, u, 512 * h : 512 * (h + 1), e],
-                                start=(u == 0 and e == 0),
-                                stop=(u == 1 and e == 1),
-                            )
-                    nc.vector.reduce_max(out=row_max[:, h : h + 1], in_=s_bank[:], axis=AXIS.X)
-                    s_banks.append(s_bank)
-                neg_max = soft.tile([P, 1], F32)
+
+        s_banks, row_max, neg_max, e_rows, half_sums, row_scale = {}, {}, {}, {}, {}, {}
+        e_bank, e_grouped, e_codes, e_scales, o_bank = {}, {}, {}, {}, {}
+
+        def live(r):
+            return 0 <= r < ROUNDS
+
+        def scores_and_transposes(r, h, jobs):
+            share = len(jobs) // 4
+            if live(r):
+                s_bank = psum.tile([P, 512], F32, tag="bank")
+                s_banks[r, h] = s_bank
+            for step in range(4):
+                u, e = divmod(step, 2)
+                if live(r):
+                    j, qt = divmod(r, ROW_TILES)
+                    nc.tensor.matmul(
+                        out=s_banks[r, h][:],
+                        lhsT=q_steps[:, u, qt * P : (qt + 1) * P, e],
+                        rhs=k_steps[j][:, u, 512 * h : 512 * (h + 1), e],
+                        start=(step == 0),
+                        stop=(step == 3),
+                    )
+                for job in jobs[share * step : share * (step + 1)]:
+                    nc.tensor.transpose(*job)
+
+        def half_maximum(r, h):
+            if not live(r):
+                return
+            if h == 0:
+                maxima = stats.tile([P, 2], F32)
+                row_max[r] = maxima
+            nc.vector.reduce_max(out=row_max[r][:, h : h + 1], in_=s_banks[r, h][:], axis=AXIS.X)
+            if h == 1:
+                shift = stats.tile([P, 1], F32)
+                neg_max[r] = shift
                 nc.vector.tensor_scalar(
-                    out=neg_max[:], in0=row_max[:, 0:1], scalar1=row_max[:, 1:2], scalar2=-SCORE_SCALE,
+                    out=shift[:], in0=row_max[r][:, 0:1], scalar1=row_max[r][:, 1:2], scalar2=-SCORE_SCALE,
                     op0=ALU.max, op1=ALU.mult,
                 )
-                e_rows = soft.tile([P, ROW_TILES, P], BF16)
-                half_sums = soft.tile([P, 2], F32)
-                for h in range(2):
-                    nc.scalar.activation(
-                        out=e_rows[:, 4 * h : 4 * h + 4, :].rearrange("p t r -> p (t r)"),
-                        in_=s_banks[h][:],
-                        func=ACT.Exp,
-                        bias=neg_max[:, 0:1],
-                        scale=SCORE_SCALE,
-                        accum_out=half_sums[:, h : h + 1],
-                    )
-                row_scale = soft.tile([P, 1], F32)
-                nc.vector.reduce_sum(out=row_scale[:], in_=half_sums[:], axis=AXIS.X)
-                nc.vector.reciprocal(out=row_scale[:], in_=row_scale[:])
-                e_bank = psum.tile([P, ROW_TILES, P], BF16, tag="bank")
-                for kt in range(ROW_TILES):
-                    nc.tensor.transpose(e_bank[:, kt, :], e_rows[:, kt, :], ident_bf16[:])
-                e_grouped = soft.tile([P, KEY_PASSES, P, 4], BF16, align_bytes=64)
-                nc.scalar.copy(out=e_grouped[:], in_=e_bank[:].rearrange("p (g t) r -> p g r t", g=KEY_PASSES))
-                e_codes = soft.tile([P, KEY_PASSES, P], U32, align_bytes=64)
-                e_scales = soft.tile([P, KEY_PASSES, P], U8, align_bytes=64)
-                nc.vector.quantize_mx(
-                    out=e_codes[:].rearrange("p g r -> p (g r)").bitcast(FP8X4),
-                    scales=e_scales[:].rearrange("p g r -> p (g r)"),
-                    in_=e_grouped[:].rearrange("p g r t -> p (g r t)"),
+
+        def exponentials(r):
+            if not live(r):
+                return
+            e_tile = soft.tile([P, ROW_TILES, P], BF16)
+            e_rows[r] = e_tile
+            sums = stats.tile([P, 2], F32)
+            half_sums[r] = sums
+            for h in range(2):
+                nc.scalar.activation(
+                    out=e_tile[:, PACK * h : PACK * (h + 1), :].rearrange("p t r -> p (t r)"),
+                    in_=s_banks[r, h][:],
+                    func=ACT.Exp,
+                    bias=neg_max[r][:, 0:1],
+                    scale=SCORE_SCALE,
+                    accum_out=sums[:, h : h + 1],
                 )
-                o_bank = psum.tile([P, WIDTH], F32, tag="bank")
-                for g in range(KEY_PASSES):
-                    nc.tensor.matmul_mx(
-                        out=o_bank[:],
-                        lhsT=e_codes[:, g, :].bitcast(FP8X4),
-                        lhsT_scale=e_scales[:, g, :],
-                        rhs=v_codes[:, g, :].bitcast(FP8X4),
-                        rhs_scale=v_scales[:, g, :],
-                        start=(g == 0),
-                        stop=(g == KEY_PASSES - 1),
-                    )
-                o_rows = stage.tile([P, WIDTH], F32)
-                nc.vector.tensor_scalar(out=o_rows[:], in0=o_bank[:], scalar1=row_scale[:, 0:1], scalar2=None, op0=ALU.mult)
-                nc.sync.dma_start(out=out_views[j][:, qt, :], in_=o_rows[:])
+
+        def reciprocal_of_row_sum(r):
+            if not live(r):
+                return
+            scale = stats.tile([P, 1], F32)
+            row_scale[r] = scale
+            nc.vector.reduce_sum(out=scale[:], in_=half_sums[r][:], axis=AXIS.X)
+            nc.vector.reciprocal(out=scale[:], in_=scale[:])
+
+        def e_transposes(r):
+            if not live(r):
+                return []
+            bank = psum.tile([P, ROW_TILES, P], BF16, tag="bank")
+            e_bank[r] = bank
+            return [(bank[:, kt, :], e_rows[r][:, kt, :], ident_bf16[:]) for kt in range(ROW_TILES)]
+
+        def group_e(r):
+            if not live(r):
+                return
+            grouped = soft.tile([P, KEY_PASSES, P, PACK], BF16, align_bytes=64)
+            e_grouped[r] = grouped
+            nc.scalar.copy(out=grouped[:], in_=e_bank[r][:].rearrange("p (g t) r -> p g r t", g=KEY_PASSES))
+
+        def quantise_e(r):
+            if not live(r):
+                return
+            codes = soft.tile([P, KEY_PASSES, P], U32, align_bytes=64)
+            scales = soft.tile([P, KEY_PASSES, P], U8, align_bytes=64)
+            e_codes[r], e_scales[r] = codes, scales
+            nc.vector.quantize_mx(
+                out=codes[:].rearrange("p g r -> p (g r)").bitcast(FP8X4),
+                scales=scales[:].rearrange("p g r -> p (g r)"),
+                in_=e_grouped[r][:].rearrange("p g r t -> p (g r t)"),
+            )
+
+        def attend(r):
+            if not live(r):
+                return
+            bank = psum.tile([P, WIDTH], F32, tag="bank")
+            o_bank[r] = bank
+            for g in range(KEY_PASSES):
+                nc.tensor.matmul_mx(
+                    out=bank[:],
+                    lhsT=e_codes[r][:, g, :].bitcast(FP8X4),
+                    lhsT_scale=e_scales[r][:, g, :],
+                    rhs=v_codes[:, g, :].bitcast(FP8X4),
+                    rhs_scale=v_scales[:, g, :],
+                    start=(g == 0),
+                    stop=(g == KEY_PASSES - 1),
+                )
+
+        def normalise_and_store(r):
+            if not live(r):
+                return
+            j, qt = divmod(r, ROW_TILES)
+            o_rows = stage.tile([P, WIDTH], F32)
+            nc.vector.tensor_scalar(
+                out=o_rows[:], in0=o_bank[r][:], scalar1=row_scale[r][:, 0:1], scalar2=None, op0=ALU.mult
+            )
+            nc.sync.dma_start(out=out_views[j][:, qt, :], in_=o_rows[:])
+
+        for i in range(ROUNDS + 4):
+            quantise_e(i - 3)
+            normalise_and_store(i - 4)
+            exponentials(i - 1)
+            scores_and_transposes(i, 0, e_transposes(i - 2))
+            half_maximum(i, 0)
+            reciprocal_of_row_sum(i - 1)
+            group_e(i - 2)
+            if i < len(side_banks):
+                rows, flipped, pair = side_banks[i]
+                side_bank, side_jobs = word_transposes(rows[:].bitcast(F32), pair)
+            else:
+                side_jobs = []
+            scores_and_transposes(i, 1, side_jobs)
+            half_maximum(i, 1)
+            if i < len(side_banks):
+                nc.vector.tensor_copy(
+                    out=score_operand_slot(flipped, pair), in_=side_bank[:].rearrange("p k u r -> p u k r")
+                )
+            attend(i - 3)

@@ -19,9 +19,17 @@ TOKENS = 1024
 WIDTH = 512
 STREAMS = 3
 ROW_TILES = TOKENS // P
+ROW_PAIRS = ROW_TILES // 2
 KEY_PASSES = TOKENS // (P * PACK)
 ROUNDS = 2 * ROW_TILES
+SCORE_MATMULS = 8
 SCORE_SCALE = 1.0 / math.sqrt(WIDTH)
+
+SIDE_BANKS_PER_STEP = 3
+FIRST_PROJECT_STEP = (2 * STREAMS + 2 * STREAMS) // SIDE_BANKS_PER_STEP
+KEY_TILES_PER_STEP = 2
+FIRST_V_QUANTISE_STEP = FIRST_PROJECT_STEP + ROW_TILES // KEY_TILES_PER_STEP + 1
+SECOND_PART_LAG = ROW_TILES + 2
 
 FLOPS = 2 * TOKENS * STREAMS * WIDTH * WIDTH + 4 * 2 * TOKENS * TOKENS * WIDTH
 
@@ -33,9 +41,9 @@ def tile_sc_attn_pa_kernel(tc, q, k1, k2, sp, om1, om2, v_w, v_b, out_0, out_1):
         const = ctx.enter_context(tc.tile_pool(name="const", bufs=1))
         inputs = ctx.enter_context(tc.tile_pool(name="inputs", bufs=1))
         keep = ctx.enter_context(tc.tile_pool(name="keep", bufs=1))
-        stage = ctx.enter_context(tc.tile_pool(name="stage", bufs=4))
-        soft = ctx.enter_context(tc.tile_pool(name="soft", bufs=3))
-        stats = ctx.enter_context(tc.tile_pool(name="stats", bufs=6))
+        side = ctx.enter_context(tc.tile_pool(name="side", bufs=2 * SIDE_BANKS_PER_STEP))
+        e_pool = ctx.enter_context(tc.tile_pool(name="e_pool", bufs=ROW_TILES + 2))
+        pairs = ctx.enter_context(tc.tile_pool(name="pairs", bufs=4))
         psum = ctx.enter_context(tc.psum_pool(name="psum", bufs=8))
 
         ident_words = const.tile([P, P], F32)
@@ -45,20 +53,10 @@ def tile_sc_attn_pa_kernel(tc, q, k1, k2, sp, om1, om2, v_w, v_b, out_0, out_1):
         bias_rows = const.tile([P, WIDTH], BF16)
         nc.gpsimd.dma_start(out=bias_rows[:], in_=v_b.partition_broadcast(P))
 
-        w_rows = inputs.tile([P, WIDTH // P, STREAMS * WIDTH], BF16)
-        w_view = v_w.rearrange("(t p) f -> p t f", p=P)
-        for s in range(STREAMS):
-            features = slice(s * WIDTH, (s + 1) * WIDTH)
-            nc.sync.dma_start(out=w_rows[:, :, features], in_=w_view[:, :, features])
-
-        def load_key_rows(rows, x, g):
-            view = x.rearrange("(g p t) c -> p g t c", g=KEY_PASSES, p=P, t=PACK)
+        def load_key_rows(rows, source, g):
+            view = source.rearrange("(g p t) c -> p g t c", g=KEY_PASSES, p=P, t=PACK)
             nc.sync.dma_start(out=rows[:, PACK * g : PACK * (g + 1), :], in_=view[:, g])
 
-        stream_rows = [inputs.tile([P, ROW_TILES, WIDTH], BF16, name="stream_rows%d" % s) for s in range(STREAMS)]
-        for g in range(KEY_PASSES):
-            for s, x in enumerate((sp, om1, om2)):
-                load_key_rows(stream_rows[s], x, g)
         k_rows = [inputs.tile([P, ROW_TILES, WIDTH], BF16, name="k_rows%d" % j) for j in range(2)]
         for g in range(KEY_PASSES):
             load_key_rows(k_rows[0], k1, g)
@@ -67,6 +65,15 @@ def tile_sc_attn_pa_kernel(tc, q, k1, k2, sp, om1, om2, v_w, v_b, out_0, out_1):
         for half in range(2):
             tiles = slice(half * ROW_TILES // 2, (half + 1) * ROW_TILES // 2)
             nc.sync.dma_start(out=q_rows[:, tiles, :], in_=q_view[:, tiles, :])
+        w_rows = inputs.tile([P, WIDTH // P, STREAMS * WIDTH], BF16)
+        w_view = v_w.rearrange("(t p) f -> p t f", p=P)
+        for s in range(STREAMS):
+            features = slice(s * WIDTH, (s + 1) * WIDTH)
+            nc.sync.dma_start(out=w_rows[:, :, features], in_=w_view[:, :, features])
+        stream_rows = [inputs.tile([P, ROW_TILES, WIDTH], BF16, name="stream_rows%d" % s) for s in range(STREAMS)]
+        for g in range(KEY_PASSES):
+            for s, source in enumerate((sp, om1, om2)):
+                load_key_rows(stream_rows[s], source, g)
         for g in range(KEY_PASSES):
             load_key_rows(k_rows[1], k2, g)
 
@@ -79,46 +86,83 @@ def tile_sc_attn_pa_kernel(tc, q, k1, k2, sp, om1, om2, v_w, v_b, out_0, out_1):
             ]
             return bank, jobs
 
-        def flip_and_quantise(words, pair, codes, scales):
-            bank, jobs = word_transposes(words, pair)
-            for job in jobs:
-                nc.tensor.transpose(*job)
-            grouped = stage.tile([P, 2 * P * PACK], BF16, align_bytes=64)
-            nc.scalar.copy(
-                out=grouped[:].bitcast(F32).rearrange("p (k r u) -> p k r u", k=2, u=2),
-                in_=bank[:].rearrange("p k u r -> p k r u"),
-            )
-            cols = slice(2 * P * pair, 2 * P * (pair + 1))
-            nc.vector.quantize_mx(out=codes[:, cols].bitcast(FP8X4), scales=scales[:, cols], in_=grouped[:])
+        qT = keep.tile([P, 2, 2 * TOKENS], BF16)
+        kT = [keep.tile([P, 2, 2 * TOKENS], BF16, name="kT%d" % j) for j in range(2)]
 
         def score_operand_slot(flipped, pair):
             rows = slice(2 * P * pair, 2 * P * (pair + 1))
             return flipped[:].bitcast(F32)[:, :, rows].rearrange("p u (k r) -> p u k r", k=2)
 
+        first_banks = [(k_rows[0], kT[0], pair) for pair in range(ROW_PAIRS)]
+        first_banks += [(q_rows, qT, pair) for pair in range(ROW_PAIRS)]
+        for number, (rows, flipped, pair) in enumerate(first_banks):
+            bank, jobs = word_transposes(rows[:].bitcast(F32), pair)
+            for job in jobs:
+                nc.tensor.transpose(*job)
+            if number % 2 == 0:
+                nc.vector.tensor_copy(out=score_operand_slot(flipped, pair), in_=bank[:].rearrange("p k u r -> p u k r"))
+            else:
+                nc.scalar.copy(out=score_operand_slot(flipped, pair), in_=bank[:].rearrange("p k u r -> p u k r"))
+
+        q_steps = qT[:].rearrange("p u (r e) -> p u r e", e=2)
+        k_steps = [kT[j][:].rearrange("p u (r e) -> p u r e", e=2) for j in range(2)]
+
         w_codes = keep.tile([P, STREAMS, WIDTH], U32, align_bytes=64)
         w_scales = keep.tile([P, STREAMS, WIDTH], U8, align_bytes=64)
         om_codes = keep.tile([P, STREAMS, TOKENS], U32, align_bytes=64)
         om_scales = keep.tile([P, STREAMS, TOKENS], U8, align_bytes=64)
+
+        side_banks = []
+        w_words = w_rows[:].bitcast(F32)
+        for s in range(STREAMS):
+            for pair in range(WIDTH // P // 2):
+                words = w_words[:, :, (WIDTH // 2) * s : (WIDTH // 2) * (s + 1)]
+                side_banks.append((words, pair, (w_codes[:, s, :], w_scales[:, s, :])))
+        for g in range(KEY_PASSES):
+            for s in range(STREAMS):
+                for pair in range(2 * g, 2 * g + 2):
+                    side_banks.append((stream_rows[s][:].bitcast(F32), pair, (om_codes[:, s, :], om_scales[:, s, :])))
+        for pair in range(ROW_PAIRS):
+            side_banks.append((k_rows[1][:].bitcast(F32), pair, None))
+
+        def empty_side_bank(bank, pair, target):
+            if target is None:
+                nc.scalar.copy(out=score_operand_slot(kT[1], pair), in_=bank[:].rearrange("p k u r -> p u k r"))
+                return None
+            grouped = side.tile([P, 2 * P * PACK], BF16, align_bytes=64)
+            nc.scalar.copy(
+                out=grouped[:].bitcast(F32).rearrange("p (k r u) -> p k r u", k=2, u=2),
+                in_=bank[:].rearrange("p k u r -> p k r u"),
+            )
+            return grouped
+
+        def quantise_side_bank(grouped, pair, target):
+            codes, scales = target
+            cols = slice(2 * P * pair, 2 * P * (pair + 1))
+            nc.vector.quantize_mx(out=codes[:, cols].bitcast(FP8X4), scales=scales[:, cols], in_=grouped[:])
+
         v_rows = keep.tile([P, ROW_TILES, WIDTH], BF16)
         v_grouped = keep.tile([P, KEY_PASSES, WIDTH, PACK], BF16, align_bytes=64)
         v_codes = keep.tile([P, KEY_PASSES, WIDTH], U32, align_bytes=64)
         v_scales = keep.tile([P, KEY_PASSES, WIDTH], U8, align_bytes=64)
 
-        def project_keys(g):
-            for kt in range(PACK * g, PACK * (g + 1)):
-                keys = slice(kt * P, (kt + 1) * P)
-                v_bank = psum.tile([P, WIDTH], F32, tag="bank")
-                for s in range(STREAMS):
-                    nc.tensor.matmul_mx(
-                        out=v_bank[:],
-                        lhsT=om_codes[:, s, keys].bitcast(FP8X4),
-                        lhsT_scale=om_scales[:, s, keys],
-                        rhs=w_codes[:, s, :].bitcast(FP8X4),
-                        rhs_scale=w_scales[:, s, :],
-                        start=(s == 0),
-                        stop=(s == STREAMS - 1),
-                    )
-                nc.vector.tensor_tensor(out=v_rows[:, kt, :], in0=v_bank[:], in1=bias_rows[:], op=ALU.add)
+        def project_key_tile(kt):
+            keys = slice(kt * P, (kt + 1) * P)
+            v_bank = psum.tile([P, WIDTH], F32, tag="bank")
+            for s in range(STREAMS):
+                nc.tensor.matmul_mx(
+                    out=v_bank[:],
+                    lhsT=om_codes[:, s, keys].bitcast(FP8X4),
+                    lhsT_scale=om_scales[:, s, keys],
+                    rhs=w_codes[:, s, :].bitcast(FP8X4),
+                    rhs_scale=w_scales[:, s, :],
+                    start=(s == 0),
+                    stop=(s == STREAMS - 1),
+                )
+            return v_bank
+
+        def add_bias(kt, v_bank):
+            nc.vector.tensor_tensor(out=v_rows[:, kt, :], in0=v_bank[:], in1=bias_rows[:], op=ALU.add)
 
         def quantise_v(g):
             nc.vector.tensor_copy(
@@ -130,120 +174,84 @@ def tile_sc_attn_pa_kernel(tc, q, k1, k2, sp, om1, om2, v_w, v_b, out_0, out_1):
                 in_=v_grouped[:, g].rearrange("p c t -> p (c t)"),
             )
 
-        w_words = w_rows[:].bitcast(F32)
-        for s in range(STREAMS):
-            for pair in range(WIDTH // P // 2):
-                flip_and_quantise(
-                    w_words[:, :, (WIDTH // 2) * s : (WIDTH // 2) * (s + 1)], pair, w_codes[:, s, :], w_scales[:, s, :]
-                )
-        for g in range(KEY_PASSES):
-            for s in range(STREAMS):
-                for pair in range(2 * g, 2 * g + 2):
-                    flip_and_quantise(stream_rows[s][:].bitcast(F32), pair, om_codes[:, s, :], om_scales[:, s, :])
-            if g > 0:
-                quantise_v(g - 1)
-            project_keys(g)
-
-        qT = keep.tile([P, 2, 2 * TOKENS], BF16)
-        kT = [keep.tile([P, 2, 2 * TOKENS], BF16, name="kT%d" % j) for j in range(2)]
-        first_banks = [(k_rows[0], kT[0], pair) for pair in range(ROW_TILES // 2)] + [(q_rows, qT, 0)]
-        side_banks = [(q_rows, qT, pair) for pair in range(1, ROW_TILES // 2)]
-        side_banks += [(k_rows[1], kT[1], pair) for pair in range(ROW_TILES // 2)]
-        for rows, flipped, pair in first_banks:
-            bank, jobs = word_transposes(rows[:].bitcast(F32), pair)
-            for job in jobs:
-                nc.tensor.transpose(*job)
-            nc.scalar.copy(out=score_operand_slot(flipped, pair), in_=bank[:].rearrange("p k u r -> p u k r"))
-        quantise_v(KEY_PASSES - 1)
-
-        q_steps = qT[:].rearrange("p u (r e) -> p u r e", e=2)
-        k_steps = [kT[j][:].rearrange("p u (r e) -> p u r e", e=2) for j in range(2)]
-        out_views = [o.rearrange("(p t) c -> p t c", t=ROW_TILES) for o in (out_0, out_1)]
-
-        s_banks, row_max, neg_max, e_rows, half_sums, row_scale = {}, {}, {}, {}, {}, {}
-        e_bank, e_grouped, e_codes, e_scales, o_bank = {}, {}, {}, {}, {}
+        row_max = keep.tile([P, ROUNDS, 2], F32)
+        neg_max = keep.tile([P, ROUNDS], F32)
+        half_sums = keep.tile([P, ROUNDS, 2], F32)
+        row_scale = keep.tile([P, ROUNDS], F32)
+        s_banks, e_rows = {}, {}
 
         def live(r):
             return 0 <= r < ROUNDS
 
-        def scores_and_transposes(r, h, jobs):
-            share = len(jobs) // 4
-            if live(r):
-                s_bank = psum.tile([P, 512], F32, tag="bank")
-                s_banks[r, h] = s_bank
-            for step in range(4):
-                u, e = divmod(step, 2)
+        def scores_and_transposes(r, jobs):
+            for m in range(SCORE_MATMULS):
+                h, quarter = divmod(m, 4)
+                u, e = divmod(quarter, 2)
                 if live(r):
                     j, qt = divmod(r, ROW_TILES)
+                    if quarter == 0:
+                        s_bank = psum.tile([P, 512], F32, tag="bank")
+                        s_banks[r, h] = s_bank
                     nc.tensor.matmul(
                         out=s_banks[r, h][:],
                         lhsT=q_steps[:, u, qt * P : (qt + 1) * P, e],
                         rhs=k_steps[j][:, u, 512 * h : 512 * (h + 1), e],
-                        start=(step == 0),
-                        stop=(step == 3),
+                        start=(quarter == 0),
+                        stop=(quarter == 3),
                     )
-                for job in jobs[share * step : share * (step + 1)]:
+                for job in jobs[m * len(jobs) // SCORE_MATMULS : (m + 1) * len(jobs) // SCORE_MATMULS]:
                     nc.tensor.transpose(*job)
 
-        def half_maximum(r, h):
+        def row_maximum(r):
             if not live(r):
                 return
-            if h == 0:
-                maxima = stats.tile([P, 2], F32)
-                row_max[r] = maxima
-            nc.vector.reduce_max(out=row_max[r][:, h : h + 1], in_=s_banks[r, h][:], axis=AXIS.X)
-            if h == 1:
-                shift = stats.tile([P, 1], F32)
-                neg_max[r] = shift
-                nc.vector.tensor_scalar(
-                    out=shift[:], in0=row_max[r][:, 0:1], scalar1=row_max[r][:, 1:2], scalar2=-SCORE_SCALE,
-                    op0=ALU.max, op1=ALU.mult,
-                )
+            for h in range(2):
+                nc.vector.reduce_max(out=row_max[:, r, h : h + 1], in_=s_banks[r, h][:], axis=AXIS.X)
+            nc.vector.tensor_scalar(
+                out=neg_max[:, r : r + 1], in0=row_max[:, r, 0:1], scalar1=row_max[:, r, 1:2], scalar2=-SCORE_SCALE,
+                op0=ALU.max, op1=ALU.mult,
+            )
 
         def exponentials(r):
             if not live(r):
                 return
-            e_tile = soft.tile([P, ROW_TILES, P], BF16)
+            e_tile = e_pool.tile([P, ROW_TILES, P], BF16)
             e_rows[r] = e_tile
-            sums = stats.tile([P, 2], F32)
-            half_sums[r] = sums
             for h in range(2):
                 nc.scalar.activation(
                     out=e_tile[:, PACK * h : PACK * (h + 1), :].rearrange("p t r -> p (t r)"),
                     in_=s_banks[r, h][:],
                     func=ACT.Exp,
-                    bias=neg_max[r][:, 0:1],
+                    bias=neg_max[:, r : r + 1],
                     scale=SCORE_SCALE,
-                    accum_out=sums[:, h : h + 1],
+                    accum_out=half_sums[:, r, h : h + 1],
                 )
 
         def reciprocal_of_row_sum(r):
             if not live(r):
                 return
-            scale = stats.tile([P, 1], F32)
-            row_scale[r] = scale
-            nc.vector.reduce_sum(out=scale[:], in_=half_sums[r][:], axis=AXIS.X)
-            nc.vector.reciprocal(out=scale[:], in_=scale[:])
+            nc.vector.reduce_sum(out=row_scale[:, r : r + 1], in_=half_sums[:, r, :], axis=AXIS.X)
+            nc.vector.reciprocal(out=row_scale[:, r : r + 1], in_=row_scale[:, r : r + 1])
+
+        out_views = [o.rearrange("(p t) c -> p t c", t=ROW_TILES) for o in (out_0, out_1)]
+        e_bank, e_grouped, e_codes, e_scales, o_bank = {}, {}, {}, {}, {}
+
+        def both_rounds(x):
+            return [x, x + ROW_TILES] if 0 <= x < ROW_TILES else []
 
         def e_transposes(r):
-            if not live(r):
-                return []
             bank = psum.tile([P, ROW_TILES, P], BF16, tag="bank")
             e_bank[r] = bank
             return [(bank[:, kt, :], e_rows[r][:, kt, :], ident_bf16[:]) for kt in range(ROW_TILES)]
 
         def group_e(r):
-            if not live(r):
-                return
-            grouped = soft.tile([P, KEY_PASSES, P, PACK], BF16, align_bytes=64)
+            grouped = pairs.tile([P, KEY_PASSES, P, PACK], BF16, align_bytes=64)
             e_grouped[r] = grouped
             nc.scalar.copy(out=grouped[:], in_=e_bank[r][:].rearrange("p (g t) r -> p g r t", g=KEY_PASSES))
 
         def quantise_e(r):
-            if not live(r):
-                return
-            codes = soft.tile([P, KEY_PASSES, P], U32, align_bytes=64)
-            scales = soft.tile([P, KEY_PASSES, P], U8, align_bytes=64)
+            codes = pairs.tile([P, KEY_PASSES, P], U32, align_bytes=64)
+            scales = pairs.tile([P, KEY_PASSES, P], U8, align_bytes=64)
             e_codes[r], e_scales[r] = codes, scales
             nc.vector.quantize_mx(
                 out=codes[:].rearrange("p g r -> p (g r)").bitcast(FP8X4),
@@ -252,8 +260,6 @@ def tile_sc_attn_pa_kernel(tc, q, k1, k2, sp, om1, om2, v_w, v_b, out_0, out_1):
             )
 
         def attend(r):
-            if not live(r):
-                return
             bank = psum.tile([P, WIDTH], F32, tag="bank")
             o_bank[r] = bank
             for g in range(KEY_PASSES):
@@ -268,32 +274,56 @@ def tile_sc_attn_pa_kernel(tc, q, k1, k2, sp, om1, om2, v_w, v_b, out_0, out_1):
                 )
 
         def normalise_and_store(r):
-            if not live(r):
-                return
             j, qt = divmod(r, ROW_TILES)
-            o_rows = stage.tile([P, WIDTH], F32)
+            o_rows = pairs.tile([P, WIDTH], F32)
             nc.vector.tensor_scalar(
-                out=o_rows[:], in0=o_bank[r][:], scalar1=row_scale[r][:, 0:1], scalar2=None, op0=ALU.mult
+                out=o_rows[:], in0=o_bank[r][:], scalar1=row_scale[:, r : r + 1], scalar2=None, op0=ALU.mult
             )
             nc.sync.dma_start(out=out_views[j][:, qt, :], in_=o_rows[:])
 
-        for i in range(ROUNDS + 4):
-            quantise_e(i - 3)
-            normalise_and_store(i - 4)
+        to_quantise = []
+        to_bias = []
+        for i in range(SECOND_PART_LAG + ROW_TILES + 2):
+            x = i - SECOND_PART_LAG
+
+            for kt, v_bank in to_bias:
+                add_bias(kt, v_bank)
+            for grouped, pair, target in to_quantise:
+                quantise_side_bank(grouped, pair, target)
+            if 0 <= i - FIRST_V_QUANTISE_STEP < KEY_PASSES:
+                quantise_v(i - FIRST_V_QUANTISE_STEP)
+            for r in both_rounds(x - 1):
+                quantise_e(r)
+            for r in both_rounds(x - 2):
+                normalise_and_store(r)
+
             exponentials(i - 1)
-            scores_and_transposes(i, 0, e_transposes(i - 2))
-            half_maximum(i, 0)
+
+            jobs = []
+            for r in both_rounds(x):
+                jobs += e_transposes(r)
+            opened = []
+            for words, pair, target in side_banks[SIDE_BANKS_PER_STEP * i : SIDE_BANKS_PER_STEP * (i + 1)]:
+                bank, bank_jobs = word_transposes(words, pair)
+                jobs += bank_jobs
+                opened.append((bank, pair, target))
+            scores_and_transposes(i, jobs)
+
+            row_maximum(i)
             reciprocal_of_row_sum(i - 1)
-            group_e(i - 2)
-            if i < len(side_banks):
-                rows, flipped, pair = side_banks[i]
-                side_bank, side_jobs = word_transposes(rows[:].bitcast(F32), pair)
-            else:
-                side_jobs = []
-            scores_and_transposes(i, 1, side_jobs)
-            half_maximum(i, 1)
-            if i < len(side_banks):
-                nc.vector.tensor_copy(
-                    out=score_operand_slot(flipped, pair), in_=side_bank[:].rearrange("p k u r -> p u k r")
-                )
-            attend(i - 3)
+
+            for r in both_rounds(x):
+                group_e(r)
+            to_quantise = []
+            for bank, pair, target in opened:
+                grouped = empty_side_bank(bank, pair, target)
+                if target is not None:
+                    to_quantise.append((grouped, pair, target))
+
+            for r in both_rounds(x - 1):
+                attend(r)
+            to_bias = []
+            first_kt = KEY_TILES_PER_STEP * (i - FIRST_PROJECT_STEP)
+            if 0 <= first_kt < ROW_TILES:
+                for kt in range(first_kt, first_kt + KEY_TILES_PER_STEP):
+                    to_bias.append((kt, project_key_tile(kt)))

@@ -25,8 +25,8 @@ ROUNDS = 2 * ROW_TILES
 SCORE_MATMULS = 8
 SCORE_SCALE = 1.0 / math.sqrt(WIDTH)
 
-SIDE_BANKS_PER_STEP = 3
-FIRST_PROJECT_STEP = (2 * STREAMS + 2 * STREAMS) // SIDE_BANKS_PER_STEP
+SIDE_BANKS_PER_STEP = 4
+FIRST_PROJECT_STEP = -(-(ROW_PAIRS - 1 + 2 * STREAMS + 2 * STREAMS) // SIDE_BANKS_PER_STEP)
 KEY_TILES_PER_STEP = 2
 FIRST_V_QUANTISE_STEP = FIRST_PROJECT_STEP + ROW_TILES // KEY_TILES_PER_STEP + 1
 SECOND_PART_LAG = ROW_TILES + 2
@@ -62,8 +62,7 @@ def tile_sc_attn_pa_kernel(tc, q, k1, k2, sp, om1, om2, v_w, v_b, out_0, out_1):
             load_key_rows(k_rows[0], k1, g)
         q_rows = inputs.tile([P, ROW_TILES, WIDTH], BF16)
         q_view = q.rearrange("(p t) c -> p t c", t=ROW_TILES)
-        for half in range(2):
-            tiles = slice(half * ROW_TILES // 2, (half + 1) * ROW_TILES // 2)
+        for tiles in (slice(0, 2), slice(2, ROW_TILES)):
             nc.sync.dma_start(out=q_rows[:, tiles, :], in_=q_view[:, tiles, :])
         w_rows = inputs.tile([P, WIDTH // P, STREAMS * WIDTH], BF16)
         w_view = v_w.rearrange("(t p) f -> p t f", p=P)
@@ -93,8 +92,7 @@ def tile_sc_attn_pa_kernel(tc, q, k1, k2, sp, om1, om2, v_w, v_b, out_0, out_1):
             rows = slice(2 * P * pair, 2 * P * (pair + 1))
             return flipped[:].bitcast(F32)[:, :, rows].rearrange("p u (k r) -> p u k r", k=2)
 
-        first_banks = [(k_rows[0], kT[0], pair) for pair in range(ROW_PAIRS)]
-        first_banks += [(q_rows, qT, pair) for pair in range(ROW_PAIRS)]
+        first_banks = [(k_rows[0], kT[0], pair) for pair in range(ROW_PAIRS)] + [(q_rows, qT, 0)]
         for number, (rows, flipped, pair) in enumerate(first_banks):
             bank, jobs = word_transposes(rows[:].bitcast(F32), pair)
             for job in jobs:
@@ -112,22 +110,22 @@ def tile_sc_attn_pa_kernel(tc, q, k1, k2, sp, om1, om2, v_w, v_b, out_0, out_1):
         om_codes = keep.tile([P, STREAMS, TOKENS], U32, align_bytes=64)
         om_scales = keep.tile([P, STREAMS, TOKENS], U8, align_bytes=64)
 
-        side_banks = []
+        side_banks = [(q_rows[:].bitcast(F32), pair, qT, None) for pair in range(1, ROW_PAIRS)]
         w_words = w_rows[:].bitcast(F32)
         for s in range(STREAMS):
             for pair in range(WIDTH // P // 2):
                 words = w_words[:, :, (WIDTH // 2) * s : (WIDTH // 2) * (s + 1)]
-                side_banks.append((words, pair, (w_codes[:, s, :], w_scales[:, s, :])))
+                side_banks.append((words, pair, None, (w_codes[:, s, :], w_scales[:, s, :])))
         for g in range(KEY_PASSES):
             for s in range(STREAMS):
                 for pair in range(2 * g, 2 * g + 2):
-                    side_banks.append((stream_rows[s][:].bitcast(F32), pair, (om_codes[:, s, :], om_scales[:, s, :])))
-        for pair in range(ROW_PAIRS):
-            side_banks.append((k_rows[1][:].bitcast(F32), pair, None))
+                    words = stream_rows[s][:].bitcast(F32)
+                    side_banks.append((words, pair, None, (om_codes[:, s, :], om_scales[:, s, :])))
+        side_banks += [(k_rows[1][:].bitcast(F32), pair, kT[1], None) for pair in range(ROW_PAIRS)]
 
-        def empty_side_bank(bank, pair, target):
-            if target is None:
-                nc.scalar.copy(out=score_operand_slot(kT[1], pair), in_=bank[:].rearrange("p k u r -> p u k r"))
+        def empty_side_bank(bank, pair, flipped):
+            if flipped is not None:
+                nc.scalar.copy(out=score_operand_slot(flipped, pair), in_=bank[:].rearrange("p k u r -> p u k r"))
                 return None
             grouped = side.tile([P, 2 * P * PACK], BF16, align_bytes=64)
             nc.scalar.copy(
@@ -184,6 +182,7 @@ def tile_sc_attn_pa_kernel(tc, q, k1, k2, sp, om1, om2, v_w, v_b, out_0, out_1):
             return 0 <= r < ROUNDS
 
         def scores_and_transposes(r, jobs):
+            gaps = SCORE_MATMULS - 1
             for m in range(SCORE_MATMULS):
                 h, quarter = divmod(m, 4)
                 u, e = divmod(quarter, 2)
@@ -199,18 +198,18 @@ def tile_sc_attn_pa_kernel(tc, q, k1, k2, sp, om1, om2, v_w, v_b, out_0, out_1):
                         start=(quarter == 0),
                         stop=(quarter == 3),
                     )
-                for job in jobs[m * len(jobs) // SCORE_MATMULS : (m + 1) * len(jobs) // SCORE_MATMULS]:
+                for job in jobs[m * len(jobs) // gaps : (m + 1) * len(jobs) // gaps]:
                     nc.tensor.transpose(*job)
 
-        def row_maximum(r):
+        def half_maximum(r, h):
             if not live(r):
                 return
-            for h in range(2):
-                nc.vector.reduce_max(out=row_max[:, r, h : h + 1], in_=s_banks[r, h][:], axis=AXIS.X)
-            nc.vector.tensor_scalar(
-                out=neg_max[:, r : r + 1], in0=row_max[:, r, 0:1], scalar1=row_max[:, r, 1:2], scalar2=-SCORE_SCALE,
-                op0=ALU.max, op1=ALU.mult,
-            )
+            nc.vector.reduce_max(out=row_max[:, r, h : h + 1], in_=s_banks[r, h][:], axis=AXIS.X)
+            if h == 1:
+                nc.vector.tensor_scalar(
+                    out=neg_max[:, r : r + 1], in0=row_max[:, r, 0:1], scalar1=row_max[:, r, 1:2],
+                    scalar2=-SCORE_SCALE, op0=ALU.max, op1=ALU.mult,
+                )
 
         def exponentials(r):
             if not live(r):
@@ -247,7 +246,10 @@ def tile_sc_attn_pa_kernel(tc, q, k1, k2, sp, om1, om2, v_w, v_b, out_0, out_1):
         def group_e(r):
             grouped = pairs.tile([P, KEY_PASSES, P, PACK], BF16, align_bytes=64)
             e_grouped[r] = grouped
-            nc.scalar.copy(out=grouped[:], in_=e_bank[r][:].rearrange("p (g t) r -> p g r t", g=KEY_PASSES))
+            if r < ROW_TILES:
+                nc.vector.tensor_copy(out=grouped[:], in_=e_bank[r][:].rearrange("p (g t) r -> p g r t", g=KEY_PASSES))
+            else:
+                nc.scalar.copy(out=grouped[:], in_=e_bank[r][:].rearrange("p (g t) r -> p g r t", g=KEY_PASSES))
 
         def quantise_e(r):
             codes = pairs.tile([P, KEY_PASSES, P], U32, align_bytes=64)
@@ -276,9 +278,12 @@ def tile_sc_attn_pa_kernel(tc, q, k1, k2, sp, om1, om2, v_w, v_b, out_0, out_1):
         def normalise_and_store(r):
             j, qt = divmod(r, ROW_TILES)
             o_rows = pairs.tile([P, WIDTH], F32)
-            nc.vector.tensor_scalar(
-                out=o_rows[:], in0=o_bank[r][:], scalar1=row_scale[:, r : r + 1], scalar2=None, op0=ALU.mult
-            )
+            if r < ROW_TILES:
+                nc.scalar.activation(out=o_rows[:], in_=o_bank[r][:], func=ACT.Copy, scale=row_scale[:, r : r + 1])
+            else:
+                nc.vector.tensor_scalar(
+                    out=o_rows[:], in0=o_bank[r][:], scalar1=row_scale[:, r : r + 1], scalar2=None, op0=ALU.mult
+                )
             nc.sync.dma_start(out=out_views[j][:, qt, :], in_=o_rows[:])
 
         to_quantise = []
@@ -292,31 +297,30 @@ def tile_sc_attn_pa_kernel(tc, q, k1, k2, sp, om1, om2, v_w, v_b, out_0, out_1):
                 quantise_side_bank(grouped, pair, target)
             if 0 <= i - FIRST_V_QUANTISE_STEP < KEY_PASSES:
                 quantise_v(i - FIRST_V_QUANTISE_STEP)
+            exponentials(i - 1)
             for r in both_rounds(x - 1):
                 quantise_e(r)
             for r in both_rounds(x - 2):
                 normalise_and_store(r)
 
-            exponentials(i - 1)
-
             jobs = []
             for r in both_rounds(x):
                 jobs += e_transposes(r)
             opened = []
-            for words, pair, target in side_banks[SIDE_BANKS_PER_STEP * i : SIDE_BANKS_PER_STEP * (i + 1)]:
+            for words, pair, flipped, target in side_banks[SIDE_BANKS_PER_STEP * i : SIDE_BANKS_PER_STEP * (i + 1)]:
                 bank, bank_jobs = word_transposes(words, pair)
                 jobs += bank_jobs
-                opened.append((bank, pair, target))
+                opened.append((bank, pair, flipped, target))
             scores_and_transposes(i, jobs)
 
-            row_maximum(i)
-            reciprocal_of_row_sum(i - 1)
-
+            half_maximum(i, 0)
             for r in both_rounds(x):
                 group_e(r)
+            half_maximum(i, 1)
+            reciprocal_of_row_sum(i - 1)
             to_quantise = []
-            for bank, pair, target in opened:
-                grouped = empty_side_bank(bank, pair, target)
+            for bank, pair, flipped, target in opened:
+                grouped = empty_side_bank(bank, pair, flipped)
                 if target is not None:
                     to_quantise.append((grouped, pair, target))
 

@@ -25,11 +25,13 @@ ROUNDS = 2 * ROW_TILES
 SCORE_MATMULS = 8
 SCORE_SCALE = 1.0 / math.sqrt(WIDTH)
 
-SIDE_BANKS_PER_STEP = 4
-FIRST_PROJECT_STEP = -(-(ROW_PAIRS - 1 + 2 * STREAMS + 2 * STREAMS) // SIDE_BANKS_PER_STEP)
-KEY_TILES_PER_STEP = 2
-FIRST_V_QUANTISE_STEP = FIRST_PROJECT_STEP + ROW_TILES // KEY_TILES_PER_STEP + 1
-SECOND_PART_LAG = ROW_TILES + 2
+SIDE_BANKS_PER_STEP = 3
+V_BANKS = KEY_PASSES * (WIDTH // P)
+V_BANKS_PER_STEP = 2
+FIRST_PROJECT_STEP = (2 * STREAMS + 2 * STREAMS) // SIDE_BANKS_PER_STEP
+V_READY_STEP = FIRST_PROJECT_STEP + V_BANKS // V_BANKS_PER_STEP
+ATTENTION_1_LAG = V_READY_STEP
+ATTENTION_2_LAG = 2
 
 FLOPS = 2 * TOKENS * STREAMS * WIDTH * WIDTH + 4 * 2 * TOKENS * TOKENS * WIDTH
 
@@ -42,7 +44,7 @@ def tile_sc_attn_pa_kernel(tc, q, k1, k2, sp, om1, om2, v_w, v_b, out_0, out_1):
         inputs = ctx.enter_context(tc.tile_pool(name="inputs", bufs=1))
         keep = ctx.enter_context(tc.tile_pool(name="keep", bufs=1))
         side = ctx.enter_context(tc.tile_pool(name="side", bufs=2 * SIDE_BANKS_PER_STEP))
-        e_pool = ctx.enter_context(tc.tile_pool(name="e_pool", bufs=ROW_TILES + 2))
+        e_pool = ctx.enter_context(tc.tile_pool(name="e_pool", bufs=ATTENTION_1_LAG + 2))
         pairs = ctx.enter_context(tc.tile_pool(name="pairs", bufs=4))
         psum = ctx.enter_context(tc.psum_pool(name="psum", bufs=8))
 
@@ -62,7 +64,8 @@ def tile_sc_attn_pa_kernel(tc, q, k1, k2, sp, om1, om2, v_w, v_b, out_0, out_1):
             load_key_rows(k_rows[0], k1, g)
         q_rows = inputs.tile([P, ROW_TILES, WIDTH], BF16)
         q_view = q.rearrange("(p t) c -> p t c", t=ROW_TILES)
-        for tiles in (slice(0, 2), slice(2, ROW_TILES)):
+        for half in range(2):
+            tiles = slice(half * ROW_TILES // 2, (half + 1) * ROW_TILES // 2)
             nc.sync.dma_start(out=q_rows[:, tiles, :], in_=q_view[:, tiles, :])
         w_rows = inputs.tile([P, WIDTH // P, STREAMS * WIDTH], BF16)
         w_view = v_w.rearrange("(t p) f -> p t f", p=P)
@@ -92,7 +95,8 @@ def tile_sc_attn_pa_kernel(tc, q, k1, k2, sp, om1, om2, v_w, v_b, out_0, out_1):
             rows = slice(2 * P * pair, 2 * P * (pair + 1))
             return flipped[:].bitcast(F32)[:, :, rows].rearrange("p u (k r) -> p u k r", k=2)
 
-        first_banks = [(k_rows[0], kT[0], pair) for pair in range(ROW_PAIRS)] + [(q_rows, qT, 0)]
+        first_banks = [(k_rows[0], kT[0], pair) for pair in range(ROW_PAIRS)]
+        first_banks += [(q_rows, qT, pair) for pair in range(ROW_PAIRS)]
         for number, (rows, flipped, pair) in enumerate(first_banks):
             bank, jobs = word_transposes(rows[:].bitcast(F32), pair)
             for job in jobs:
@@ -110,22 +114,22 @@ def tile_sc_attn_pa_kernel(tc, q, k1, k2, sp, om1, om2, v_w, v_b, out_0, out_1):
         om_codes = keep.tile([P, STREAMS, TOKENS], U32, align_bytes=64)
         om_scales = keep.tile([P, STREAMS, TOKENS], U8, align_bytes=64)
 
-        side_banks = [(q_rows[:].bitcast(F32), pair, qT, None) for pair in range(1, ROW_PAIRS)]
+        side_banks = []
         w_words = w_rows[:].bitcast(F32)
         for s in range(STREAMS):
             for pair in range(WIDTH // P // 2):
                 words = w_words[:, :, (WIDTH // 2) * s : (WIDTH // 2) * (s + 1)]
-                side_banks.append((words, pair, None, (w_codes[:, s, :], w_scales[:, s, :])))
+                side_banks.append((words, pair, (w_codes[:, s, :], w_scales[:, s, :])))
         for g in range(KEY_PASSES):
             for s in range(STREAMS):
                 for pair in range(2 * g, 2 * g + 2):
-                    words = stream_rows[s][:].bitcast(F32)
-                    side_banks.append((words, pair, None, (om_codes[:, s, :], om_scales[:, s, :])))
-        side_banks += [(k_rows[1][:].bitcast(F32), pair, kT[1], None) for pair in range(ROW_PAIRS)]
+                    side_banks.append((stream_rows[s][:].bitcast(F32), pair, (om_codes[:, s, :], om_scales[:, s, :])))
+        for pair in range(ROW_PAIRS):
+            side_banks.append((k_rows[1][:].bitcast(F32), pair, None))
 
-        def empty_side_bank(bank, pair, flipped):
-            if flipped is not None:
-                nc.scalar.copy(out=score_operand_slot(flipped, pair), in_=bank[:].rearrange("p k u r -> p u k r"))
+        def empty_side_bank(bank, pair, target):
+            if target is None:
+                nc.scalar.copy(out=score_operand_slot(kT[1], pair), in_=bank[:].rearrange("p k u r -> p u k r"))
                 return None
             grouped = side.tile([P, 2 * P * PACK], BF16, align_bytes=64)
             nc.scalar.copy(
@@ -139,33 +143,39 @@ def tile_sc_attn_pa_kernel(tc, q, k1, k2, sp, om1, om2, v_w, v_b, out_0, out_1):
             cols = slice(2 * P * pair, 2 * P * (pair + 1))
             nc.vector.quantize_mx(out=codes[:, cols].bitcast(FP8X4), scales=scales[:, cols], in_=grouped[:])
 
-        v_rows = keep.tile([P, ROW_TILES, WIDTH], BF16)
         v_grouped = keep.tile([P, KEY_PASSES, WIDTH, PACK], BF16, align_bytes=64)
         v_codes = keep.tile([P, KEY_PASSES, WIDTH], U32, align_bytes=64)
         v_scales = keep.tile([P, KEY_PASSES, WIDTH], U8, align_bytes=64)
 
-        def project_key_tile(kt):
-            keys = slice(kt * P, (kt + 1) * P)
-            v_bank = psum.tile([P, WIDTH], F32, tag="bank")
-            for s in range(STREAMS):
-                nc.tensor.matmul_mx(
-                    out=v_bank[:],
-                    lhsT=om_codes[:, s, keys].bitcast(FP8X4),
-                    lhsT_scale=om_scales[:, s, keys],
-                    rhs=w_codes[:, s, :].bitcast(FP8X4),
-                    rhs_scale=w_scales[:, s, :],
-                    start=(s == 0),
-                    stop=(s == STREAMS - 1),
-                )
+        def project(number):
+            g, block = divmod(number, WIDTH // P)
+            channels = slice(block * P, (block + 1) * P)
+            v_bank = psum.tile([P, PACK, P], F32, tag="bank")
+            for t in range(PACK):
+                keys = slice((PACK * g + t) * P, (PACK * g + t + 1) * P)
+                for s in range(STREAMS):
+                    nc.tensor.matmul_mx(
+                        out=v_bank[:, t, :],
+                        lhsT=om_codes[:, s, keys].bitcast(FP8X4),
+                        lhsT_scale=om_scales[:, s, keys],
+                        rhs=w_codes[:, s, channels].bitcast(FP8X4),
+                        rhs_scale=w_scales[:, s, channels],
+                        start=(s == 0),
+                        stop=(s == STREAMS - 1),
+                    )
             return v_bank
 
-        def add_bias(kt, v_bank):
-            nc.vector.tensor_tensor(out=v_rows[:, kt, :], in0=v_bank[:], in1=bias_rows[:], op=ALU.add)
+        def add_bias(number, v_bank):
+            g, block = divmod(number, WIDTH // P)
+            channels = slice(block * P, (block + 1) * P)
+            nc.vector.tensor_tensor(
+                out=v_grouped[:, g, channels, :],
+                in0=v_bank[:].rearrange("p t c -> p c t"),
+                in1=bias_rows[:, channels].unsqueeze(2).to_broadcast([P, P, PACK]),
+                op=ALU.add,
+            )
 
         def quantise_v(g):
-            nc.vector.tensor_copy(
-                out=v_grouped[:, g], in_=v_rows[:, PACK * g : PACK * (g + 1), :].rearrange("p t c -> p c t")
-            )
             nc.vector.quantize_mx(
                 out=v_codes[:, g, :].bitcast(FP8X4),
                 scales=v_scales[:, g, :],
@@ -201,15 +211,15 @@ def tile_sc_attn_pa_kernel(tc, q, k1, k2, sp, om1, om2, v_w, v_b, out_0, out_1):
                 for job in jobs[m * len(jobs) // gaps : (m + 1) * len(jobs) // gaps]:
                     nc.tensor.transpose(*job)
 
-        def half_maximum(r, h):
+        def row_maximum(r):
             if not live(r):
                 return
-            nc.vector.reduce_max(out=row_max[:, r, h : h + 1], in_=s_banks[r, h][:], axis=AXIS.X)
-            if h == 1:
-                nc.vector.tensor_scalar(
-                    out=neg_max[:, r : r + 1], in0=row_max[:, r, 0:1], scalar1=row_max[:, r, 1:2],
-                    scalar2=-SCORE_SCALE, op0=ALU.max, op1=ALU.mult,
-                )
+            for h in range(2):
+                nc.vector.reduce_max(out=row_max[:, r, h : h + 1], in_=s_banks[r, h][:], axis=AXIS.X)
+            nc.vector.tensor_scalar(
+                out=neg_max[:, r : r + 1], in0=row_max[:, r, 0:1], scalar1=row_max[:, r, 1:2], scalar2=-SCORE_SCALE,
+                op0=ALU.max, op1=ALU.mult,
+            )
 
         def exponentials(r):
             if not live(r):
@@ -235,8 +245,13 @@ def tile_sc_attn_pa_kernel(tc, q, k1, k2, sp, om1, om2, v_w, v_b, out_0, out_1):
         out_views = [o.rearrange("(p t) c -> p t c", t=ROW_TILES) for o in (out_0, out_1)]
         e_bank, e_grouped, e_codes, e_scales, o_bank = {}, {}, {}, {}, {}
 
-        def both_rounds(x):
-            return [x, x + ROW_TILES] if 0 <= x < ROW_TILES else []
+        def rounds_flipped_in(step):
+            rounds = []
+            if 0 <= step - ATTENTION_1_LAG < ROW_TILES:
+                rounds.append(step - ATTENTION_1_LAG)
+            if ROW_TILES <= step - ATTENTION_2_LAG < ROUNDS:
+                rounds.append(step - ATTENTION_2_LAG)
+            return rounds
 
         def e_transposes(r):
             bank = psum.tile([P, ROW_TILES, P], BF16, tag="bank")
@@ -246,10 +261,7 @@ def tile_sc_attn_pa_kernel(tc, q, k1, k2, sp, om1, om2, v_w, v_b, out_0, out_1):
         def group_e(r):
             grouped = pairs.tile([P, KEY_PASSES, P, PACK], BF16, align_bytes=64)
             e_grouped[r] = grouped
-            if r < ROW_TILES:
-                nc.vector.tensor_copy(out=grouped[:], in_=e_bank[r][:].rearrange("p (g t) r -> p g r t", g=KEY_PASSES))
-            else:
-                nc.scalar.copy(out=grouped[:], in_=e_bank[r][:].rearrange("p (g t) r -> p g r t", g=KEY_PASSES))
+            nc.scalar.copy(out=grouped[:], in_=e_bank[r][:].rearrange("p (g t) r -> p g r t", g=KEY_PASSES))
 
         def quantise_e(r):
             codes = pairs.tile([P, KEY_PASSES, P], U32, align_bytes=64)
@@ -278,56 +290,52 @@ def tile_sc_attn_pa_kernel(tc, q, k1, k2, sp, om1, om2, v_w, v_b, out_0, out_1):
         def normalise_and_store(r):
             j, qt = divmod(r, ROW_TILES)
             o_rows = pairs.tile([P, WIDTH], F32)
-            if r < ROW_TILES:
-                nc.scalar.activation(out=o_rows[:], in_=o_bank[r][:], func=ACT.Copy, scale=row_scale[:, r : r + 1])
-            else:
-                nc.vector.tensor_scalar(
-                    out=o_rows[:], in0=o_bank[r][:], scalar1=row_scale[:, r : r + 1], scalar2=None, op0=ALU.mult
-                )
+            nc.vector.tensor_scalar(
+                out=o_rows[:], in0=o_bank[r][:], scalar1=row_scale[:, r : r + 1], scalar2=None, op0=ALU.mult
+            )
             nc.sync.dma_start(out=out_views[j][:, qt, :], in_=o_rows[:])
 
         to_quantise = []
         to_bias = []
-        for i in range(SECOND_PART_LAG + ROW_TILES + 2):
-            x = i - SECOND_PART_LAG
-
-            for kt, v_bank in to_bias:
-                add_bias(kt, v_bank)
+        for i in range(ROUNDS + ATTENTION_2_LAG + 2):
+            for number, v_bank in to_bias:
+                add_bias(number, v_bank)
+                if (number + 1) % (WIDTH // P) == 0:
+                    quantise_v(number // (WIDTH // P))
             for grouped, pair, target in to_quantise:
                 quantise_side_bank(grouped, pair, target)
-            if 0 <= i - FIRST_V_QUANTISE_STEP < KEY_PASSES:
-                quantise_v(i - FIRST_V_QUANTISE_STEP)
-            exponentials(i - 1)
-            for r in both_rounds(x - 1):
+            for r in rounds_flipped_in(i - 1):
                 quantise_e(r)
-            for r in both_rounds(x - 2):
+            for r in rounds_flipped_in(i - 2):
                 normalise_and_store(r)
 
+            exponentials(i - 1)
+
             jobs = []
-            for r in both_rounds(x):
+            for r in rounds_flipped_in(i):
                 jobs += e_transposes(r)
             opened = []
-            for words, pair, flipped, target in side_banks[SIDE_BANKS_PER_STEP * i : SIDE_BANKS_PER_STEP * (i + 1)]:
+            for words, pair, target in side_banks[SIDE_BANKS_PER_STEP * i : SIDE_BANKS_PER_STEP * (i + 1)]:
                 bank, bank_jobs = word_transposes(words, pair)
                 jobs += bank_jobs
-                opened.append((bank, pair, flipped, target))
+                opened.append((bank, pair, target))
             scores_and_transposes(i, jobs)
 
-            half_maximum(i, 0)
-            for r in both_rounds(x):
-                group_e(r)
-            half_maximum(i, 1)
+            row_maximum(i)
             reciprocal_of_row_sum(i - 1)
+
+            for r in rounds_flipped_in(i):
+                group_e(r)
             to_quantise = []
-            for bank, pair, flipped, target in opened:
-                grouped = empty_side_bank(bank, pair, flipped)
+            for bank, pair, target in opened:
+                grouped = empty_side_bank(bank, pair, target)
                 if target is not None:
                     to_quantise.append((grouped, pair, target))
 
-            for r in both_rounds(x - 1):
+            for r in rounds_flipped_in(i - 1):
                 attend(r)
             to_bias = []
-            first_kt = KEY_TILES_PER_STEP * (i - FIRST_PROJECT_STEP)
-            if 0 <= first_kt < ROW_TILES:
-                for kt in range(first_kt, first_kt + KEY_TILES_PER_STEP):
-                    to_bias.append((kt, project_key_tile(kt)))
+            first_bank = V_BANKS_PER_STEP * (i - FIRST_PROJECT_STEP)
+            if 0 <= first_bank < V_BANKS:
+                for number in range(first_bank, first_bank + V_BANKS_PER_STEP):
+                    to_bias.append((number, project(number)))

@@ -50,8 +50,6 @@ def tile_sc_attn_pa_kernel(tc, q, k1, k2, sp, om1, om2, v_w, v_b, out_0, out_1):
 
         ident_words = const.tile([P, P], F32)
         make_identity(nc, ident_words[:])
-        ident_bf16 = const.tile([P, P], BF16)
-        make_identity(nc, ident_bf16[:])
         bias_rows = const.tile([P, WIDTH], BF16)
         nc.gpsimd.dma_start(out=bias_rows[:], in_=v_b.partition_broadcast(P))
 
@@ -92,19 +90,24 @@ def tile_sc_attn_pa_kernel(tc, q, k1, k2, sp, om1, om2, v_w, v_b, out_0, out_1):
         kT = [keep.tile([P, 2, 2 * TOKENS], BF16, name="kT%d" % j) for j in range(2)]
 
         def score_operand_slot(flipped, pair):
-            rows = slice(2 * P * pair, 2 * P * (pair + 1))
-            return flipped[:].bitcast(F32)[:, :, rows].rearrange("p u (k r) -> p u k r", k=2)
+            return flipped[:].bitcast(F32)[:, :, 2 * P * pair : 2 * P * (pair + 1)]
 
-        first_banks = [(k_rows[0], kT[0], pair) for pair in range(ROW_PAIRS)]
-        first_banks += [(q_rows, qT, pair) for pair in range(ROW_PAIRS)]
-        for number, (rows, flipped, pair) in enumerate(first_banks):
+        def query_slot(pair):
+            return score_operand_slot(qT, pair).rearrange("p u (k r) -> p u k r", k=2)
+
+        def key_slot(j, pair):
+            return score_operand_slot(kT[j], pair).rearrange("p u (r k) -> p u r k", k=2)
+
+        first_banks = [(k_rows[0], pair, key_slot(0, pair), "p k u r -> p u r k") for pair in range(ROW_PAIRS)]
+        first_banks += [(q_rows, pair, query_slot(pair), "p k u r -> p u k r") for pair in range(ROW_PAIRS)]
+        for number, (rows, pair, slot, order) in enumerate(first_banks):
             bank, jobs = word_transposes(rows[:].bitcast(F32), pair)
             for job in jobs:
                 nc.tensor.transpose(*job)
             if number % 2 == 0:
-                nc.vector.tensor_copy(out=score_operand_slot(flipped, pair), in_=bank[:].rearrange("p k u r -> p u k r"))
+                nc.vector.tensor_copy(out=slot, in_=bank[:].rearrange(order))
             else:
-                nc.scalar.copy(out=score_operand_slot(flipped, pair), in_=bank[:].rearrange("p k u r -> p u k r"))
+                nc.scalar.copy(out=slot, in_=bank[:].rearrange(order))
 
         q_steps = qT[:].rearrange("p u (r e) -> p u r e", e=2)
         k_steps = [kT[j][:].rearrange("p u (r e) -> p u r e", e=2) for j in range(2)]
@@ -129,7 +132,7 @@ def tile_sc_attn_pa_kernel(tc, q, k1, k2, sp, om1, om2, v_w, v_b, out_0, out_1):
 
         def empty_side_bank(bank, pair, target):
             if target is None:
-                nc.scalar.copy(out=score_operand_slot(kT[1], pair), in_=bank[:].rearrange("p k u r -> p u k r"))
+                nc.scalar.copy(out=key_slot(1, pair), in_=bank[:].rearrange("p k u r -> p u r k"))
                 return None
             grouped = side.tile([P, 2 * P * PACK], BF16, align_bytes=64)
             nc.scalar.copy(
@@ -224,11 +227,11 @@ def tile_sc_attn_pa_kernel(tc, q, k1, k2, sp, om1, om2, v_w, v_b, out_0, out_1):
         def exponentials(r):
             if not live(r):
                 return
-            e_tile = e_pool.tile([P, ROW_TILES, P], BF16)
+            e_tile = e_pool.tile([P, TOKENS], BF16)
             e_rows[r] = e_tile
             for h in range(2):
                 nc.scalar.activation(
-                    out=e_tile[:, PACK * h : PACK * (h + 1), :].rearrange("p t r -> p (t r)"),
+                    out=e_tile[:, 512 * h : 512 * (h + 1)],
                     in_=s_banks[r, h][:],
                     func=ACT.Exp,
                     bias=neg_max[:, r : r + 1],
@@ -254,14 +257,18 @@ def tile_sc_attn_pa_kernel(tc, q, k1, k2, sp, om1, om2, v_w, v_b, out_0, out_1):
             return rounds
 
         def e_transposes(r):
-            bank = psum.tile([P, ROW_TILES, P], BF16, tag="bank")
+            bank = psum.tile([P, KEY_PASSES, 2, P], F32, tag="bank")
             e_bank[r] = bank
-            return [(bank[:, kt, :], e_rows[r][:, kt, :], ident_bf16[:]) for kt in range(ROW_TILES)]
+            words = e_rows[r][:].bitcast(F32).rearrange("p (g u k) -> p g u k", g=KEY_PASSES, u=2)
+            return [(bank[:, g, u, :], words[:, g, u, :], ident_words[:]) for g in range(KEY_PASSES) for u in range(2)]
 
         def group_e(r):
             grouped = pairs.tile([P, KEY_PASSES, P, PACK], BF16, align_bytes=64)
             e_grouped[r] = grouped
-            nc.scalar.copy(out=grouped[:], in_=e_bank[r][:].rearrange("p (g t) r -> p g r t", g=KEY_PASSES))
+            nc.scalar.copy(
+                out=grouped[:].bitcast(F32),
+                in_=e_bank[r][:].rearrange("p g u r -> p g r u"),
+            )
 
         def quantise_e(r):
             codes = pairs.tile([P, KEY_PASSES, P], U32, align_bytes=64)

@@ -28,7 +28,10 @@ SCORE_SCALE = 1.0 / math.sqrt(WIDTH)
 SIDE_BANKS_PER_STEP = 3
 V_BANKS = KEY_PASSES * (WIDTH // P)
 V_BANKS_PER_STEP = 2
-FIRST_PROJECT_STEP = (2 * STREAMS + 2 * STREAMS) // SIDE_BANKS_PER_STEP
+FIRST_PROJECT_STEP = 5
+FIRST_FLIP_STEP = 8
+FLIPS = {8: 1, 9: 1, 10: 2, 11: 1, 12: 2, 13: 1, 14: 2, 15: 1}
+LAST_STEP = 21
 V_READY_STEP = FIRST_PROJECT_STEP + V_BANKS // V_BANKS_PER_STEP
 ATTENTION_1_LAG = V_READY_STEP
 ATTENTION_2_LAG = 2
@@ -43,9 +46,9 @@ def tile_sc_attn_pa_kernel(tc, q, k1, k2, sp, om1, om2, v_w, v_b, out_0, out_1):
         const = ctx.enter_context(tc.tile_pool(name="const", bufs=1))
         inputs = ctx.enter_context(tc.tile_pool(name="inputs", bufs=1))
         keep = ctx.enter_context(tc.tile_pool(name="keep", bufs=1))
-        side = ctx.enter_context(tc.tile_pool(name="side", bufs=2 * SIDE_BANKS_PER_STEP))
-        e_pool = ctx.enter_context(tc.tile_pool(name="e_pool", bufs=ATTENTION_1_LAG + 2))
-        pairs = ctx.enter_context(tc.tile_pool(name="pairs", bufs=4))
+        side = ctx.enter_context(tc.tile_pool(name="side", bufs=8))
+        e_pool = ctx.enter_context(tc.tile_pool(name="e_pool", bufs=ROUNDS))
+        pairs = ctx.enter_context(tc.tile_pool(name="pairs", bufs=6))
         psum = ctx.enter_context(tc.psum_pool(name="psum", bufs=8))
 
         ident_words = const.tile([P, P], F32)
@@ -58,18 +61,31 @@ def tile_sc_attn_pa_kernel(tc, q, k1, k2, sp, om1, om2, v_w, v_b, out_0, out_1):
             nc.sync.dma_start(out=rows[:, PACK * g : PACK * (g + 1), :], in_=view[:, g])
 
         k_rows = [inputs.tile([P, ROW_TILES, WIDTH], BF16, name="k_rows%d" % j) for j in range(2)]
-        for g in range(KEY_PASSES):
-            load_key_rows(k_rows[0], k1, g)
+        k_views = [k.rearrange("(g p t) c -> p g t c", g=KEY_PASSES, p=P, t=PACK) for k in (k1, k2)]
         q_rows = inputs.tile([P, ROW_TILES, WIDTH], BF16)
         q_view = q.rearrange("(p t) c -> p t c", t=ROW_TILES)
-        for half in range(2):
-            tiles = slice(half * ROW_TILES // 2, (half + 1) * ROW_TILES // 2)
-            nc.sync.dma_start(out=q_rows[:, tiles, :], in_=q_view[:, tiles, :])
+
+        def load_key_pair(j, pair):
+            g, half = divmod(pair, 2)
+            nc.sync.dma_start(
+                out=k_rows[j][:, 2 * pair : 2 * pair + 2, :], in_=k_views[j][:, g, 2 * half : 2 * half + 2, :]
+            )
+
+        def load_query_tiles(first, last):
+            nc.sync.dma_start(out=q_rows[:, first:last, :], in_=q_view[:, first:last, :])
+
+        load_key_pair(0, 0)
+        load_query_tiles(0, 2)
+        for pair in range(1, ROW_PAIRS):
+            load_key_pair(0, pair)
+        load_query_tiles(2, 4)
         w_rows = inputs.tile([P, WIDTH // P, STREAMS * WIDTH], BF16)
         w_view = v_w.rearrange("(t p) f -> p t f", p=P)
         for s in range(STREAMS):
             features = slice(s * WIDTH, (s + 1) * WIDTH)
             nc.sync.dma_start(out=w_rows[:, :, features], in_=w_view[:, :, features])
+            if s == 1:
+                load_query_tiles(4, 8)
         stream_rows = [inputs.tile([P, ROW_TILES, WIDTH], BF16, name="stream_rows%d" % s) for s in range(STREAMS)]
         for g in range(KEY_PASSES):
             for s, source in enumerate((sp, om1, om2)):
@@ -98,16 +114,17 @@ def tile_sc_attn_pa_kernel(tc, q, k1, k2, sp, om1, om2, v_w, v_b, out_0, out_1):
         def key_slot(j, pair):
             return score_operand_slot(kT[j], pair).rearrange("p u (r k) -> p u r k", k=2)
 
-        first_banks = [(k_rows[0], pair, key_slot(0, pair), "p k u r -> p u r k") for pair in range(ROW_PAIRS)]
-        first_banks += [(q_rows, pair, query_slot(pair), "p k u r -> p u k r") for pair in range(ROW_PAIRS)]
-        for number, (rows, pair, slot, order) in enumerate(first_banks):
+        def flip_first(copy, rows, pair, slot, order):
             bank, jobs = word_transposes(rows[:].bitcast(F32), pair)
             for job in jobs:
                 nc.tensor.transpose(*job)
-            if number % 2 == 0:
-                nc.vector.tensor_copy(out=slot, in_=bank[:].rearrange(order))
-            else:
-                nc.scalar.copy(out=slot, in_=bank[:].rearrange(order))
+            copy(out=slot, in_=bank[:].rearrange(order))
+
+        def flip_k1(copy, pair):
+            flip_first(copy, k_rows[0], pair, key_slot(0, pair), "p k u r -> p u r k")
+
+        def flip_q(copy, pair):
+            flip_first(copy, q_rows, pair, query_slot(pair), "p k u r -> p u k r")
 
         q_steps = qT[:].rearrange("p u (r e) -> p u r e", e=2)
         k_steps = [kT[j][:].rearrange("p u (r e) -> p u r e", e=2) for j in range(2)]
@@ -117,25 +134,40 @@ def tile_sc_attn_pa_kernel(tc, q, k1, k2, sp, om1, om2, v_w, v_b, out_0, out_1):
         om_codes = keep.tile([P, STREAMS, TOKENS], U32, align_bytes=64)
         om_scales = keep.tile([P, STREAMS, TOKENS], U8, align_bytes=64)
 
-        side_banks = []
         w_words = w_rows[:].bitcast(F32)
-        for s in range(STREAMS):
-            for pair in range(WIDTH // P // 2):
-                words = w_words[:, :, (WIDTH // 2) * s : (WIDTH // 2) * (s + 1)]
-                side_banks.append((words, pair, (w_codes[:, s, :], w_scales[:, s, :])))
-        for g in range(KEY_PASSES):
-            for s in range(STREAMS):
-                for pair in range(2 * g, 2 * g + 2):
-                    side_banks.append((stream_rows[s][:].bitcast(F32), pair, (om_codes[:, s, :], om_scales[:, s, :])))
-        for pair in range(ROW_PAIRS):
-            side_banks.append((k_rows[1][:].bitcast(F32), pair, None))
 
-        def empty_side_bank(bank, pair, target):
-            if target is None:
-                nc.scalar.copy(out=key_slot(1, pair), in_=bank[:].rearrange("p k u r -> p u r k"))
+        def side_w(s):
+            words = w_words[:, :, (WIDTH // 2) * s : (WIDTH // 2) * (s + 1)]
+            return [(words, pair, (w_codes[:, s, :], w_scales[:, s, :]), None) for pair in range(WIDTH // P // 2)]
+
+        def side_stream(g, s):
+            return [
+                (stream_rows[s][:].bitcast(F32), pair, (om_codes[:, s, :], om_scales[:, s, :]), None)
+                for pair in range(2 * g, 2 * g + 2)
+            ]
+
+        def side_q(pair):
+            return [(q_rows[:].bitcast(F32), pair, query_slot(pair), "p k u r -> p u k r")]
+
+        def side_k2(pair):
+            return [(k_rows[1][:].bitcast(F32), pair, key_slot(1, pair), "p k u r -> p u r k")]
+
+        streams = [side_stream(g, s) for g in range(KEY_PASSES) for s in range(STREAMS)]
+        side_plan = {
+            2: side_w(2) + side_q(2),
+            3: streams[0] + streams[1][:1],
+            4: streams[1][1:] + streams[2],
+            5: side_q(3) + streams[3] + streams[4][:1],
+            6: streams[4][1:] + streams[5],
+            7: [bank for pair in range(ROW_PAIRS) for bank in side_k2(pair)],
+        }
+
+        def empty_side_bank(copy, bank, pair, target, order):
+            if order is not None:
+                copy(out=target, in_=bank[:].rearrange(order))
                 return None
             grouped = side.tile([P, 2 * P * PACK], BF16, align_bytes=64)
-            nc.scalar.copy(
+            copy(
                 out=grouped[:].bitcast(F32).rearrange("p (k r u) -> p k r u", k=2, u=2),
                 in_=bank[:].rearrange("p k u r -> p k r u"),
             )
@@ -194,23 +226,33 @@ def tile_sc_attn_pa_kernel(tc, q, k1, k2, sp, om1, om2, v_w, v_b, out_0, out_1):
         def live(r):
             return 0 <= r < ROUNDS
 
+        def open_score_bank(r, h):
+            s_bank = psum.tile([P, 512], F32, tag="bank")
+            s_banks[r, h] = s_bank
+
+        def score_matmul(r, m):
+            h, quarter = divmod(m, 4)
+            u, e = divmod(quarter, 2)
+            j, qt = divmod(r, ROW_TILES)
+            if (r, h) not in s_banks:
+                open_score_bank(r, h)
+            nc.tensor.matmul(
+                out=s_banks[r, h][:],
+                lhsT=q_steps[:, u, qt * P : (qt + 1) * P, e],
+                rhs=k_steps[j][:, u, 512 * h : 512 * (h + 1), e],
+                start=(quarter == 0),
+                stop=(quarter == 3),
+            )
+
+        def score_half(r, h):
+            for m in range(4 * h, 4 * h + 4):
+                score_matmul(r, m)
+
         def scores_and_transposes(r, jobs):
             gaps = SCORE_MATMULS - 1
             for m in range(SCORE_MATMULS):
-                h, quarter = divmod(m, 4)
-                u, e = divmod(quarter, 2)
                 if live(r):
-                    j, qt = divmod(r, ROW_TILES)
-                    if quarter == 0:
-                        s_bank = psum.tile([P, 512], F32, tag="bank")
-                        s_banks[r, h] = s_bank
-                    nc.tensor.matmul(
-                        out=s_banks[r, h][:],
-                        lhsT=q_steps[:, u, qt * P : (qt + 1) * P, e],
-                        rhs=k_steps[j][:, u, 512 * h : 512 * (h + 1), e],
-                        start=(quarter == 0),
-                        stop=(quarter == 3),
-                    )
+                    score_matmul(r, m)
                 for job in jobs[m * len(jobs) // gaps : (m + 1) * len(jobs) // gaps]:
                     nc.tensor.transpose(*job)
 
@@ -218,7 +260,13 @@ def tile_sc_attn_pa_kernel(tc, q, k1, k2, sp, om1, om2, v_w, v_b, out_0, out_1):
             if not live(r):
                 return
             for h in range(2):
-                nc.vector.reduce_max(out=row_max[:, r, h : h + 1], in_=s_banks[r, h][:], axis=AXIS.X)
+                half_maximum(r, h)
+            negate_maximum(r)
+
+        def half_maximum(r, h):
+            nc.vector.reduce_max(out=row_max[:, r, h : h + 1], in_=s_banks[r, h][:], axis=AXIS.X)
+
+        def negate_maximum(r):
             nc.vector.tensor_scalar(
                 out=neg_max[:, r : r + 1], in0=row_max[:, r, 0:1], scalar1=row_max[:, r, 1:2], scalar2=-SCORE_SCALE,
                 op0=ALU.max, op1=ALU.mult,
@@ -248,13 +296,15 @@ def tile_sc_attn_pa_kernel(tc, q, k1, k2, sp, om1, om2, v_w, v_b, out_0, out_1):
         out_views = [o.rearrange("(p t) c -> p t c", t=ROW_TILES) for o in (out_0, out_1)]
         e_bank, e_grouped, e_codes, e_scales, o_bank = {}, {}, {}, {}, {}
 
+        flips = {}
+        waiting = list(range(ROUNDS))
+        for step in range(FIRST_FLIP_STEP, LAST_STEP):
+            count = FLIPS[step] if step in FLIPS else 2
+            flips[step] = [r for r in waiting[:count] if r <= step - 1]
+            waiting = waiting[len(flips[step]) :]
+
         def rounds_flipped_in(step):
-            rounds = []
-            if 0 <= step - ATTENTION_1_LAG < ROW_TILES:
-                rounds.append(step - ATTENTION_1_LAG)
-            if ROW_TILES <= step - ATTENTION_2_LAG < ROUNDS:
-                rounds.append(step - ATTENTION_2_LAG)
-            return rounds
+            return flips.get(step, [])
 
         def e_transposes(r):
             bank = psum.tile([P, KEY_PASSES, 2, P], F32, tag="bank")
@@ -302,9 +352,43 @@ def tile_sc_attn_pa_kernel(tc, q, k1, k2, sp, om1, om2, v_w, v_b, out_0, out_1):
             )
             nc.sync.dma_start(out=out_views[j][:, qt, :], in_=o_rows[:])
 
+        def open_side_banks(banks):
+            opened, jobs = [], []
+            for words, pair, target, order in banks:
+                bank, bank_jobs = word_transposes(words, pair)
+                jobs += bank_jobs
+                opened.append((bank, pair, target, order))
+            return opened, jobs
+
+        flip_k1(nc.vector.tensor_copy, 0)
+        flip_q(nc.scalar.copy, 0)
+        flip_k1(nc.vector.tensor_copy, 1)
+        flip_k1(nc.scalar.copy, 2)
+        score_half(0, 0)
+        half_maximum(0, 0)
+        flip_k1(nc.scalar.copy, 3)
+        flip_q(nc.scalar.copy, 1)
+        open_score_bank(0, 1)
+        score_half(1, 0)
+        half_maximum(1, 0)
+        score_half(0, 1)
+        half_maximum(0, 1)
+        negate_maximum(0)
+        exponentials(0)
+        opened, jobs = open_side_banks(side_w(0) + side_w(1))
+        for n in range(4):
+            score_matmul(1, 4 + n)
+            for job in jobs[4 * n : 4 * n + 4]:
+                nc.tensor.transpose(*job)
         to_quantise = []
+        for number, (bank, pair, target, order) in enumerate(opened):
+            copy = nc.vector.tensor_copy if number % 2 == 0 else nc.scalar.copy
+            to_quantise.append((empty_side_bank(copy, bank, pair, target, order), pair, target))
+        half_maximum(1, 1)
+        negate_maximum(1)
+
         to_bias = []
-        for i in range(ROUNDS + ATTENTION_2_LAG + 2):
+        for i in range(2, LAST_STEP):
             for number, v_bank in to_bias:
                 add_bias(number, v_bank)
                 if (number + 1) % (WIDTH // P) == 0:
@@ -321,22 +405,20 @@ def tile_sc_attn_pa_kernel(tc, q, k1, k2, sp, om1, om2, v_w, v_b, out_0, out_1):
             jobs = []
             for r in rounds_flipped_in(i):
                 jobs += e_transposes(r)
-            opened = []
-            for words, pair, target in side_banks[SIDE_BANKS_PER_STEP * i : SIDE_BANKS_PER_STEP * (i + 1)]:
-                bank, bank_jobs = word_transposes(words, pair)
-                jobs += bank_jobs
-                opened.append((bank, pair, target))
-            scores_and_transposes(i, jobs)
+            opened, side_jobs = open_side_banks(side_plan.get(i, []))
+            scores_and_transposes(i, jobs + side_jobs)
 
             row_maximum(i)
+            if i == 2:
+                reciprocal_of_row_sum(0)
             reciprocal_of_row_sum(i - 1)
 
             for r in rounds_flipped_in(i):
                 group_e(r)
             to_quantise = []
-            for bank, pair, target in opened:
-                grouped = empty_side_bank(bank, pair, target)
-                if target is not None:
+            for bank, pair, target, order in opened:
+                grouped = empty_side_bank(nc.scalar.copy, bank, pair, target, order)
+                if order is None:
                     to_quantise.append((grouped, pair, target))
 
             for r in rounds_flipped_in(i - 1):

@@ -32,6 +32,8 @@ FIRST_PROJECT_STEP = 5
 FIRST_FLIP_STEP = 8
 FLIPS = {8: 1, 9: 1, 10: 2, 11: 1, 12: 2, 13: 1, 14: 2, 15: 1}
 LAST_STEP = 21
+RECIPS = {9: (0, 8), 13: (8, 12), 16: (12, 16)}
+NORM_S = ()
 V_READY_STEP = FIRST_PROJECT_STEP + V_BANKS // V_BANKS_PER_STEP
 ATTENTION_1_LAG = V_READY_STEP
 ATTENTION_2_LAG = 2
@@ -74,8 +76,8 @@ def tile_sc_attn_pa_kernel(tc, q, k1, k2, sp, om1, om2, v_w, v_b, out_0, out_1):
         def load_query_tiles(first, last):
             nc.sync.dma_start(out=q_rows[:, first:last, :], in_=q_view[:, first:last, :])
 
-        load_key_pair(0, 0)
         load_query_tiles(0, 2)
+        load_key_pair(0, 0)
         for pair in range(1, ROW_PAIRS):
             load_key_pair(0, pair)
         load_query_tiles(2, 4)
@@ -84,8 +86,7 @@ def tile_sc_attn_pa_kernel(tc, q, k1, k2, sp, om1, om2, v_w, v_b, out_0, out_1):
         for s in range(STREAMS):
             features = slice(s * WIDTH, (s + 1) * WIDTH)
             nc.sync.dma_start(out=w_rows[:, :, features], in_=w_view[:, :, features])
-            if s == 1:
-                load_query_tiles(4, 8)
+        load_query_tiles(4, 8)
         stream_rows = [inputs.tile([P, ROW_TILES, WIDTH], BF16, name="stream_rows%d" % s) for s in range(STREAMS)]
         for g in range(KEY_PASSES):
             for s, source in enumerate((sp, om1, om2)):
@@ -244,6 +245,21 @@ def tile_sc_attn_pa_kernel(tc, q, k1, k2, sp, om1, om2, v_w, v_b, out_0, out_1):
                 stop=(quarter == 3),
             )
 
+        def score_pair(r, pair):
+            h, part = divmod(pair, 2)
+            j, qt = divmod(r, ROW_TILES)
+            if (r, h) not in s_banks:
+                open_score_bank(r, h)
+            for quarter in range(4):
+                u, e = divmod(quarter, 2)
+                nc.tensor.matmul(
+                    out=s_banks[r, h][:, 256 * part : 256 * (part + 1)],
+                    lhsT=q_steps[:, u, qt * P : (qt + 1) * P, e],
+                    rhs=k_steps[j][:, u, 256 * pair : 256 * (pair + 1), e],
+                    start=(quarter == 0),
+                    stop=(quarter == 3),
+                )
+
         def score_half(r, h):
             for m in range(4 * h, 4 * h + 4):
                 score_matmul(r, m)
@@ -287,11 +303,10 @@ def tile_sc_attn_pa_kernel(tc, q, k1, k2, sp, om1, om2, v_w, v_b, out_0, out_1):
                     accum_out=half_sums[:, r, h : h + 1],
                 )
 
-        def reciprocal_of_row_sum(r):
-            if not live(r):
-                return
-            nc.vector.reduce_sum(out=row_scale[:, r : r + 1], in_=half_sums[:, r, :], axis=AXIS.X)
-            nc.vector.reciprocal(out=row_scale[:, r : r + 1], in_=row_scale[:, r : r + 1])
+        def reciprocal_of_row_sums(first, last):
+            rounds = slice(first, last)
+            nc.vector.reduce_sum(out=row_scale[:, rounds], in_=half_sums[:, rounds, :], axis=AXIS.X)
+            nc.vector.reciprocal(out=row_scale[:, rounds], in_=row_scale[:, rounds])
 
         out_views = [o.rearrange("(p t) c -> p t c", t=ROW_TILES) for o in (out_0, out_1)]
         e_bank, e_grouped, e_codes, e_scales, o_bank = {}, {}, {}, {}, {}
@@ -347,9 +362,12 @@ def tile_sc_attn_pa_kernel(tc, q, k1, k2, sp, om1, om2, v_w, v_b, out_0, out_1):
         def normalise_and_store(r):
             j, qt = divmod(r, ROW_TILES)
             o_rows = pairs.tile([P, WIDTH], F32)
-            nc.vector.tensor_scalar(
-                out=o_rows[:], in0=o_bank[r][:], scalar1=row_scale[:, r : r + 1], scalar2=None, op0=ALU.mult
-            )
+            if r not in NORM_S:
+                nc.vector.tensor_scalar(
+                    out=o_rows[:], in0=o_bank[r][:], scalar1=row_scale[:, r : r + 1], scalar2=None, op0=ALU.mult
+                )
+            else:
+                nc.scalar.activation(out=o_rows[:], in_=o_bank[r][:], func=ACT.Copy, scale=row_scale[:, r : r + 1])
             nc.sync.dma_start(out=out_views[j][:, qt, :], in_=o_rows[:])
 
         def open_side_banks(banks):
@@ -360,20 +378,24 @@ def tile_sc_attn_pa_kernel(tc, q, k1, k2, sp, om1, om2, v_w, v_b, out_0, out_1):
                 opened.append((bank, pair, target, order))
             return opened, jobs
 
-        flip_k1(nc.vector.tensor_copy, 0)
-        flip_q(nc.scalar.copy, 0)
+        flip_q(nc.vector.tensor_copy, 0)
+        flip_k1(nc.scalar.copy, 0)
         flip_k1(nc.vector.tensor_copy, 1)
+        score_pair(0, 0)
         flip_k1(nc.scalar.copy, 2)
-        score_half(0, 0)
+        score_pair(0, 1)
         half_maximum(0, 0)
         flip_k1(nc.scalar.copy, 3)
-        flip_q(nc.scalar.copy, 1)
         open_score_bank(0, 1)
+        q_bank, q_jobs = word_transposes(q_rows[:].bitcast(F32), 1)
         score_half(1, 0)
-        half_maximum(1, 0)
         score_half(0, 1)
+        half_maximum(1, 0)
         half_maximum(0, 1)
         negate_maximum(0)
+        for job in q_jobs:
+            nc.tensor.transpose(*job)
+        nc.scalar.copy(out=query_slot(1), in_=q_bank[:].rearrange("p k u r -> p u k r"))
         exponentials(0)
         opened, jobs = open_side_banks(side_w(0) + side_w(1))
         for n in range(4):
@@ -409,9 +431,8 @@ def tile_sc_attn_pa_kernel(tc, q, k1, k2, sp, om1, om2, v_w, v_b, out_0, out_1):
             scores_and_transposes(i, jobs + side_jobs)
 
             row_maximum(i)
-            if i == 2:
-                reciprocal_of_row_sum(0)
-            reciprocal_of_row_sum(i - 1)
+            if i in RECIPS:
+                reciprocal_of_row_sums(*RECIPS[i])
 
             for r in rounds_flipped_in(i):
                 group_e(r)

@@ -266,11 +266,14 @@ def tile_sc_attn_pa_kernel(tc, q, k1, k2, sp, om1, om2, v_w, v_b, out_0, out_1):
 
         def scores_and_transposes(r, jobs):
             gaps = SCORE_MATMULS - 1
+            runs = len(jobs) // 4
             for m in range(SCORE_MATMULS):
                 if live(r):
                     score_matmul(r, m)
-                for job in jobs[m * len(jobs) // gaps : (m + 1) * len(jobs) // gaps]:
-                    nc.tensor.transpose(*job)
+                for n in range(runs):
+                    if (2 * n + 1) * gaps // (2 * runs) == m:
+                        for job in jobs[4 * n : 4 * n + 4]:
+                            nc.tensor.transpose(*job)
 
         def row_maximum(r):
             if not live(r):

@@ -56,7 +56,6 @@ def tile_sc_attn_pa_kernel(tc, q, k1, k2, sp, om1, om2, v_w, v_b, out_0, out_1):
         ident_words = const.tile([P, P], F32)
         make_identity(nc, ident_words[:])
         bias_rows = const.tile([P, WIDTH], BF16)
-        nc.gpsimd.dma_start(out=bias_rows[:], in_=v_b.partition_broadcast(P))
 
         def load_key_rows(rows, source, g):
             view = source.rearrange("(g p t) c -> p g t c", g=KEY_PASSES, p=P, t=PACK)
@@ -91,6 +90,8 @@ def tile_sc_attn_pa_kernel(tc, q, k1, k2, sp, om1, om2, v_w, v_b, out_0, out_1):
         for g in range(KEY_PASSES):
             for s, source in enumerate((sp, om1, om2)):
                 load_key_rows(stream_rows[s], source, g)
+            if g == 0:
+                nc.sync.dma_start(out=bias_rows[:], in_=v_b.partition_broadcast(P))
         for g in range(KEY_PASSES):
             load_key_rows(k_rows[1], k2, g)
 

@@ -30,10 +30,11 @@ V_BANKS = KEY_PASSES * (WIDTH // P)
 V_BANKS_PER_STEP = 2
 FIRST_PROJECT_STEP = 5
 FIRST_FLIP_STEP = 8
-FLIPS = {8: 1, 9: 1, 10: 2, 11: 1, 12: 2, 13: 1, 14: 2, 15: 1}
+FLIPS = {8: 1, 9: 1, 10: 2, 11: 2, 12: 2, 13: 1, 14: 2, 15: 2}
 LAST_STEP = 21
+LAST_PIECES = 2
 RECIPS = {9: (0, 8), 13: (8, 12), 16: (12, 16)}
-NORM_S = ()
+NORM_S = (11, 13)
 V_READY_STEP = FIRST_PROJECT_STEP + V_BANKS // V_BANKS_PER_STEP
 ATTENTION_1_LAG = V_READY_STEP
 ATTENTION_2_LAG = 2
@@ -51,8 +52,11 @@ def tile_sc_attn_pa_kernel(tc, q, k1, k2, sp, om1, om2, v_w, v_b, out_0, out_1):
         side = ctx.enter_context(tc.tile_pool(name="side", bufs=8))
         e_pool = ctx.enter_context(tc.tile_pool(name="e_pool", bufs=ROUNDS))
         pairs = ctx.enter_context(tc.tile_pool(name="pairs", bufs=6))
+        outs = ctx.enter_context(tc.tile_pool(name="outs", bufs=12))
         psum = ctx.enter_context(tc.psum_pool(name="psum", bufs=8))
 
+        zeros = const.tile([P, WIDTH], BF16)
+        nc.vector.memset(zeros[:], 0.0)
         ident_words = const.tile([P, P], F32)
         make_identity(nc, ident_words[:])
         bias_rows = const.tile([P, WIDTH], BF16)
@@ -104,11 +108,11 @@ def tile_sc_attn_pa_kernel(tc, q, k1, k2, sp, om1, om2, v_w, v_b, out_0, out_1):
             ]
             return bank, jobs
 
-        qT = keep.tile([P, 2, 2 * TOKENS], BF16)
-        kT = [keep.tile([P, 2, 2 * TOKENS], BF16, name="kT%d" % j) for j in range(2)]
+        qT = keep.tile([P, ROW_PAIRS, 2, 4 * P], BF16)
+        kT = [keep.tile([P, ROW_PAIRS, 2, 4 * P], BF16, name="kT%d" % j) for j in range(2)]
 
         def score_operand_slot(flipped, pair):
-            return flipped[:].bitcast(F32)[:, :, 2 * P * pair : 2 * P * (pair + 1)]
+            return flipped[:, pair].bitcast(F32)
 
         def query_slot(pair):
             return score_operand_slot(qT, pair).rearrange("p u (k r) -> p u k r", k=2)
@@ -128,8 +132,12 @@ def tile_sc_attn_pa_kernel(tc, q, k1, k2, sp, om1, om2, v_w, v_b, out_0, out_1):
         def flip_q(copy, pair):
             flip_first(copy, q_rows, pair, query_slot(pair), "p k u r -> p u k r")
 
-        q_steps = qT[:].rearrange("p u (r e) -> p u r e", e=2)
-        k_steps = [kT[j][:].rearrange("p u (r e) -> p u r e", e=2) for j in range(2)]
+        q_steps = qT[:].rearrange("p b u (r e) -> p b u r e", e=2)
+        k_steps = [kT[j][:].rearrange("p b u (r e) -> p b u r e", e=2) for j in range(2)]
+
+        def query_operand(qt, u, e):
+            rows = slice(qt % 2 * P, (qt % 2 + 1) * P)
+            return q_steps[:, qt // 2, u, rows, e]
 
         w_codes = keep.tile([P, STREAMS, WIDTH], U32, align_bytes=64)
         w_scales = keep.tile([P, STREAMS, WIDTH], U8, align_bytes=64)
@@ -239,9 +247,9 @@ def tile_sc_attn_pa_kernel(tc, q, k1, k2, sp, om1, om2, v_w, v_b, out_0, out_1):
             if (r, h) not in s_banks:
                 open_score_bank(r, h)
             nc.tensor.matmul(
-                out=s_banks[r, h][:],
-                lhsT=q_steps[:, u, qt * P : (qt + 1) * P, e],
-                rhs=k_steps[j][:, u, 512 * h : 512 * (h + 1), e],
+                out=s_banks[r, h][:].rearrange("p (b n) -> p b n", b=2),
+                lhsT=query_operand(qt, u, e),
+                rhs=k_steps[j][:, 2 * h : 2 * h + 2, u, :, e],
                 start=(quarter == 0),
                 stop=(quarter == 3),
             )
@@ -255,8 +263,8 @@ def tile_sc_attn_pa_kernel(tc, q, k1, k2, sp, om1, om2, v_w, v_b, out_0, out_1):
                 u, e = divmod(quarter, 2)
                 nc.tensor.matmul(
                     out=s_banks[r, h][:, 256 * part : 256 * (part + 1)],
-                    lhsT=q_steps[:, u, qt * P : (qt + 1) * P, e],
-                    rhs=k_steps[j][:, u, 256 * pair : 256 * (pair + 1), e],
+                    lhsT=query_operand(qt, u, e),
+                    rhs=k_steps[j][:, pair, u, :, e],
                     start=(quarter == 0),
                     stop=(quarter == 3),
                 )
@@ -349,30 +357,39 @@ def tile_sc_attn_pa_kernel(tc, q, k1, k2, sp, om1, om2, v_w, v_b, out_0, out_1):
                 in_=e_grouped[r][:].rearrange("p g r t -> p (g r t)"),
             )
 
+        def pieces(r):
+            return LAST_PIECES if r == ROUNDS - 1 else 1
+
         def attend(r):
-            bank = psum.tile([P, WIDTH], F32, tag="bank")
-            o_bank[r] = bank
-            for g in range(KEY_PASSES):
-                nc.tensor.matmul_mx(
-                    out=bank[:],
-                    lhsT=e_codes[r][:, g, :].bitcast(FP8X4),
-                    lhsT_scale=e_scales[r][:, g, :],
-                    rhs=v_codes[:, g, :].bitcast(FP8X4),
-                    rhs_scale=v_scales[:, g, :],
-                    start=(g == 0),
-                    stop=(g == KEY_PASSES - 1),
-                )
+            width = WIDTH // pieces(r)
+            for n in range(pieces(r)):
+                channels = slice(n * width, (n + 1) * width)
+                bank = psum.tile([P, width], F32, tag="bank")
+                o_bank[r, n] = bank
+                for g in range(KEY_PASSES):
+                    nc.tensor.matmul_mx(
+                        out=bank[:],
+                        lhsT=e_codes[r][:, g, :].bitcast(FP8X4),
+                        lhsT_scale=e_scales[r][:, g, :],
+                        rhs=v_codes[:, g, channels].bitcast(FP8X4),
+                        rhs_scale=v_scales[:, g, channels],
+                        start=(g == 0),
+                        stop=(g == KEY_PASSES - 1),
+                    )
 
         def normalise_and_store(r):
             j, qt = divmod(r, ROW_TILES)
-            o_rows = pairs.tile([P, WIDTH], F32)
-            if r not in NORM_S:
-                nc.vector.tensor_scalar(
-                    out=o_rows[:], in0=o_bank[r][:], scalar1=row_scale[:, r : r + 1], scalar2=None, op0=ALU.mult
-                )
-            else:
-                nc.scalar.activation(out=o_rows[:], in_=o_bank[r][:], func=ACT.Copy, scale=row_scale[:, r : r + 1])
-            nc.sync.dma_start(out=out_views[j][:, qt, :], in_=o_rows[:])
+            width = WIDTH // pieces(r)
+            for n in range(pieces(r)):
+                channels = slice(n * width, (n + 1) * width)
+                o_rows = outs.tile([P, width], F32)
+                if r in NORM_S or n == 1:
+                    nc.scalar.activation(out=o_rows[:], in_=o_bank[r, n][:], func=ACT.Copy, scale=row_scale[:, r : r + 1])
+                else:
+                    nc.vector.tensor_scalar(
+                        out=o_rows[:], in0=o_bank[r, n][:], scalar1=row_scale[:, r : r + 1], scalar2=None, op0=ALU.mult
+                    )
+                nc.sync.dma_start(out=out_views[j][:, qt, channels], in_=o_rows[:])
 
         def open_side_banks(banks):
             opened, jobs = [], []
@@ -382,9 +399,21 @@ def tile_sc_attn_pa_kernel(tc, q, k1, k2, sp, om1, om2, v_w, v_b, out_0, out_1):
                 opened.append((bank, pair, target, order))
             return opened, jobs
 
+        warm_bank = psum.tile([P, WIDTH], F32, tag="bank")
+
+        def keep_warm(count, width):
+            for n in range(count):
+                nc.tensor.matmul(
+                    out=warm_bank[:, :width], lhsT=zeros[:, :P], rhs=zeros[:, :width], start=True, stop=True
+                )
+
+        keep_warm(4, WIDTH)
         flip_q(nc.vector.tensor_copy, 0)
+        keep_warm(2, 256)
         flip_k1(nc.scalar.copy, 0)
+        keep_warm(2, 256)
         flip_k1(nc.vector.tensor_copy, 1)
+        keep_warm(2, 256)
         score_pair(0, 0)
         flip_k1(nc.scalar.copy, 2)
         score_pair(0, 1)

from contextlib import ExitStack
import math

import concourse.mybir as mybir
from concourse.masks import make_identity

F32 = mybir.dt.float32
BF16 = mybir.dt.bfloat16
U32 = mybir.dt.uint32
U8 = mybir.dt.uint8
FP8X4 = mybir.dt.float8_e4m3fn_x4
ACT = mybir.ActivationFunctionType
ALU = mybir.AluOpType
AXIS = mybir.AxisListType

P = 128
PACK = 4
TOKENS = 1024
WIDTH = 512
STREAMS = 3
ROW_TILES = TOKENS // P
ROW_PAIRS = ROW_TILES // 2
KEY_PASSES = TOKENS // (P * PACK)
ROUNDS = 2 * ROW_TILES
SCORE_MATMULS = 8
SCORE_SCALE = 1.0 / math.sqrt(WIDTH)

SIDE_BANKS_PER_STEP = 3
V_BANKS = KEY_PASSES * (WIDTH // P)
V_BANKS_PER_STEP = 2
FIRST_PROJECT_STEP = 5
FIRST_FLIP_STEP = 8
FLIPS = {8: 1, 9: 1, 10: 2, 11: 2, 12: 2, 13: 1, 14: 2, 15: 2}
LAST_STEP = 21
LAST_PIECES = 2
RECIPS = {9: (0, 8), 13: (8, 12), 16: (12, 16)}
NORM_S = (11, 13)
V_READY_STEP = FIRST_PROJECT_STEP + V_BANKS // V_BANKS_PER_STEP
ATTENTION_1_LAG = V_READY_STEP
ATTENTION_2_LAG = 2

FLOPS = 2 * TOKENS * STREAMS * WIDTH * WIDTH + 4 * 2 * TOKENS * TOKENS * WIDTH


def tile_sc_attn_pa_kernel(tc, q, k1, k2, sp, om1, om2, v_w, v_b, out_0, out_1):
    nc = tc.nc
    with ExitStack() as ctx:
        ctx.enter_context(tc.manual_schedule())
        const = ctx.enter_context(tc.tile_pool(name="const", bufs=1))
        inputs = ctx.enter_context(tc.tile_pool(name="inputs", bufs=1))
        keep = ctx.enter_context(tc.tile_pool(name="keep", bufs=1))
        side = ctx.enter_context(tc.tile_pool(name="side", bufs=8))
        e_pool = ctx.enter_context(tc.tile_pool(name="e_pool", bufs=ROUNDS))
        pairs = ctx.enter_context(tc.tile_pool(name="pairs", bufs=6))
        outs = ctx.enter_context(tc.tile_pool(name="outs", bufs=12))
        psum = ctx.enter_context(tc.psum_pool(name="psum", bufs=8))

        zeros = const.tile([P, WIDTH], BF16)
        nc.vector.memset(zeros[:], 0.0)
        ident_words = const.tile([P, P], F32)
        make_identity(nc, ident_words[:])
        bias_rows = const.tile([P, WIDTH], BF16)

        def load_key_rows(rows, source, g):
            view = source.rearrange("(g p t) c -> p g t c", g=KEY_PASSES, p=P, t=PACK)
            nc.sync.dma_start(out=rows[:, PACK * g : PACK * (g + 1), :], in_=view[:, g])

        k_rows = [inputs.tile([P, ROW_TILES, WIDTH], BF16, name="k_rows%d" % j) for j in range(2)]
        k_views = [k.rearrange("(g p t) c -> p g t c", g=KEY_PASSES, p=P, t=PACK) for k in (k1, k2)]
        q_rows = inputs.tile([P, ROW_TILES, WIDTH], BF16)
        q_view = q.rearrange("(p t) c -> p t c", t=ROW_TILES)

        def load_key_pair(j, pair):
            g, half = divmod(pair, 2)
            nc.sync.dma_start(
                out=k_rows[j][:, 2 * pair : 2 * pair + 2, :], in_=k_views[j][:, g, 2 * half : 2 * half + 2, :]
            )

        def load_query_tiles(first, last):
            nc.sync.dma_start(out=q_rows[:, first:last, :], in_=q_view[:, first:last, :])

        load_query_tiles(0, 2)
        load_key_pair(0, 0)
        for pair in range(1, ROW_PAIRS):
            load_key_pair(0, pair)
        load_query_tiles(2, 4)
        w_rows = inputs.tile([P, WIDTH // P, STREAMS * WIDTH], BF16)
        w_view = v_w.rearrange("(t p) f -> p t f", p=P)
        for s in range(STREAMS):
            features = slice(s * WIDTH, (s + 1) * WIDTH)
            nc.sync.dma_start(out=w_rows[:, :, features], in_=w_view[:, :, features])
        load_query_tiles(4, 8)
        stream_rows = [inputs.tile([P, ROW_TILES, WIDTH], BF16, name="stream_rows%d" % s) for s in range(STREAMS)]
        for g in range(KEY_PASSES):
            for s, source in enumerate((sp, om1, om2)):
                load_key_rows(stream_rows[s], source, g)
            if g == 0:
                nc.sync.dma_start(out=bias_rows[:], in_=v_b.partition_broadcast(P))
        for g in range(KEY_PASSES):
            load_key_rows(k_rows[1], k2, g)

        def word_transposes(words, pair):
            bank = psum.tile([P, 2, 2, P], F32, tag="bank")
            jobs = [
                (bank[:, k, u, :], words[:, 2 * pair + k, u * P : (u + 1) * P], ident_words[:])
                for k in range(2)
                for u in range(2)
            ]
            return bank, jobs

        qT = keep.tile([P, ROW_PAIRS, 2, 4 * P], BF16)
        kT = [keep.tile([P, ROW_PAIRS, 2, 4 * P], BF16, name="kT%d" % j) for j in range(2)]

        def score_operand_slot(flipped, pair):
            return flipped[:, pair].bitcast(F32)

        def query_slot(pair):
            return score_operand_slot(qT, pair).rearrange("p u (k r) -> p u k r", k=2)

        def key_slot(j, pair):
            return score_operand_slot(kT[j], pair).rearrange("p u (r k) -> p u r k", k=2)

        def flip_first(copy, rows, pair, slot, order):
            bank, jobs = word_transposes(rows[:].bitcast(F32), pair)
            for job in jobs:
                nc.tensor.transpose(*job)
            copy(out=slot, in_=bank[:].rearrange(order))

        def flip_k1(copy, pair):
            flip_first(copy, k_rows[0], pair, key_slot(0, pair), "p k u r -> p u r k")

        def flip_q(copy, pair):
            flip_first(copy, q_rows, pair, query_slot(pair), "p k u r -> p u k r")

        q_steps = qT[:].rearrange("p b u (r e) -> p b u r e", e=2)
        k_steps = [kT[j][:].rearrange("p b u (r e) -> p b u r e", e=2) for j in range(2)]

        def query_operand(qt, u, e):
            rows = slice(qt % 2 * P, (qt % 2 + 1) * P)
            return q_steps[:, qt // 2, u, rows, e]

        w_codes = keep.tile([P, STREAMS, WIDTH], U32, align_bytes=64)
        w_scales = keep.tile([P, STREAMS, WIDTH], U8, align_bytes=64)
        om_codes = keep.tile([P, STREAMS, TOKENS], U32, align_bytes=64)
        om_scales = keep.tile([P, STREAMS, TOKENS], U8, align_bytes=64)

        w_words = w_rows[:].bitcast(F32)

        def side_w(s):
            words = w_words[:, :, (WIDTH // 2) * s : (WIDTH // 2) * (s + 1)]
            return [(words, pair, (w_codes[:, s, :], w_scales[:, s, :]), None) for pair in range(WIDTH // P // 2)]

        def side_stream(g, s):
            return [
                (stream_rows[s][:].bitcast(F32), pair, (om_codes[:, s, :], om_scales[:, s, :]), None)
                for pair in range(2 * g, 2 * g + 2)
            ]

        def side_q(pair):
            return [(q_rows[:].bitcast(F32), pair, query_slot(pair), "p k u r -> p u k r")]

        def side_k2(pair):
            return [(k_rows[1][:].bitcast(F32), pair, key_slot(1, pair), "p k u r -> p u r k")]

        streams = [side_stream(g, s) for g in range(KEY_PASSES) for s in range(STREAMS)]
        side_plan = {
            2: side_w(2) + side_q(2),
            3: streams[0] + streams[1][:1],
            4: streams[1][1:] + streams[2],
            5: side_q(3) + streams[3] + streams[4][:1],
            6: streams[4][1:] + streams[5],
            7: [bank for pair in range(ROW_PAIRS) for bank in side_k2(pair)],
        }

        def empty_side_bank(copy, bank, pair, target, order):
            if order is not None:
                copy(out=target, in_=bank[:].rearrange(order))
                return None
            grouped = side.tile([P, 2 * P * PACK], BF16, align_bytes=64)
            copy(
                out=grouped[:].bitcast(F32).rearrange("p (k r u) -> p k r u", k=2, u=2),
                in_=bank[:].rearrange("p k u r -> p k r u"),
            )
            return grouped

        def quantise_side_bank(grouped, pair, target):
            codes, scales = target
            cols = slice(2 * P * pair, 2 * P * (pair + 1))
            nc.vector.quantize_mx(out=codes[:, cols].bitcast(FP8X4), scales=scales[:, cols], in_=grouped[:])

        v_grouped = keep.tile([P, KEY_PASSES, WIDTH, PACK], BF16, align_bytes=64)
        v_codes = keep.tile([P, KEY_PASSES, WIDTH], U32, align_bytes=64)
        v_scales = keep.tile([P, KEY_PASSES, WIDTH], U8, align_bytes=64)

        def project(number):
            g, block = divmod(number, WIDTH // P)
            channels = slice(block * P, (block + 1) * P)
            v_bank = psum.tile([P, PACK, P], F32, tag="bank")
            for t in range(PACK):
                keys = slice((PACK * g + t) * P, (PACK * g + t + 1) * P)
                for s in range(STREAMS):
                    nc.tensor.matmul_mx(
                        out=v_bank[:, t, :],
                        lhsT=om_codes[:, s, keys].bitcast(FP8X4),
                        lhsT_scale=om_scales[:, s, keys],
                        rhs=w_codes[:, s, channels].bitcast(FP8X4),
                        rhs_scale=w_scales[:, s, channels],
                        start=(s == 0),
                        stop=(s == STREAMS - 1),
                    )
            return v_bank

        def add_bias(number, v_bank):
            g, block = divmod(number, WIDTH // P)
            channels = slice(block * P, (block + 1) * P)
            nc.vector.tensor_tensor(
                out=v_grouped[:, g, channels, :],
                in0=v_bank[:].rearrange("p t c -> p c t"),
                in1=bias_rows[:, channels].unsqueeze(2).to_broadcast([P, P, PACK]),
                op=ALU.add,
            )

        def quantise_v(g):
            nc.vector.quantize_mx(
                out=v_codes[:, g, :].bitcast(FP8X4),
                scales=v_scales[:, g, :],
                in_=v_grouped[:, g].rearrange("p c t -> p (c t)"),
            )

        row_max = keep.tile([P, ROUNDS, 2], F32)
        neg_max = keep.tile([P, ROUNDS], F32)
        half_sums = keep.tile([P, ROUNDS, 2], F32)
        row_scale = keep.tile([P, ROUNDS], F32)
        s_banks, e_rows = {}, {}

        def live(r):
            return 0 <= r < ROUNDS

        def open_score_bank(r, h):
            s_bank = psum.tile([P, 512], F32, tag="bank")
            s_banks[r, h] = s_bank

        def score_matmul(r, m):
            h, quarter = divmod(m, 4)
            u, e = divmod(quarter, 2)
            j, qt = divmod(r, ROW_TILES)
            if (r, h) not in s_banks:
                open_score_bank(r, h)
            nc.tensor.matmul(
                out=s_banks[r, h][:].rearrange("p (b n) -> p b n", b=2),
                lhsT=query_operand(qt, u, e),
                rhs=k_steps[j][:, 2 * h : 2 * h + 2, u, :, e],
                start=(quarter == 0),
                stop=(quarter == 3),
            )

        def score_pair(r, pair):
            h, part = divmod(pair, 2)
            j, qt = divmod(r, ROW_TILES)
            if (r, h) not in s_banks:
                open_score_bank(r, h)
            for quarter in range(4):
                u, e = divmod(quarter, 2)
                nc.tensor.matmul(
                    out=s_banks[r, h][:, 256 * part : 256 * (part + 1)],
                    lhsT=query_operand(qt, u, e),
                    rhs=k_steps[j][:, pair, u, :, e],
                    start=(quarter == 0),
                    stop=(quarter == 3),
                )

        def score_half(r, h):
            for m in range(4 * h, 4 * h + 4):
                score_matmul(r, m)

        def scores_and_transposes(r, jobs):
            gaps = SCORE_MATMULS - 1
            runs = len(jobs) // 4
            for m in range(SCORE_MATMULS):
                if live(r):
                    score_matmul(r, m)
                for n in range(runs):
                    if (2 * n + 1) * gaps // (2 * runs) == m:
                        for job in jobs[4 * n : 4 * n + 4]:
                            nc.tensor.transpose(*job)

        def row_maximum(r):
            if not live(r):
                return
            for h in range(2):
                half_maximum(r, h)
            negate_maximum(r)

        def half_maximum(r, h):
            nc.vector.reduce_max(out=row_max[:, r, h : h + 1], in_=s_banks[r, h][:], axis=AXIS.X)

        def negate_maximum(r):
            nc.vector.tensor_scalar(
                out=neg_max[:, r : r + 1], in0=row_max[:, r, 0:1], scalar1=row_max[:, r, 1:2], scalar2=-SCORE_SCALE,
                op0=ALU.max, op1=ALU.mult,
            )

        def exponentials(r):
            if not live(r):
                return
            e_tile = e_pool.tile([P, TOKENS], BF16)
            e_rows[r] = e_tile
            for h in range(2):
                nc.scalar.activation(
                    out=e_tile[:, 512 * h : 512 * (h + 1)],
                    in_=s_banks[r, h][:],
                    func=ACT.Exp,
                    bias=neg_max[:, r : r + 1],
                    scale=SCORE_SCALE,
                    accum_out=half_sums[:, r, h : h + 1],
                )

        def reciprocal_of_row_sums(first, last):
            rounds = slice(first, last)
            nc.vector.reduce_sum(out=row_scale[:, rounds], in_=half_sums[:, rounds, :], axis=AXIS.X)
            nc.vector.reciprocal(out=row_scale[:, rounds], in_=row_scale[:, rounds])

        out_views = [o.rearrange("(p t) c -> p t c", t=ROW_TILES) for o in (out_0, out_1)]
        e_bank, e_grouped, e_codes, e_scales, o_bank = {}, {}, {}, {}, {}

        flips = {}
        waiting = list(range(ROUNDS))
        for step in range(FIRST_FLIP_STEP, LAST_STEP):
            count = FLIPS[step] if step in FLIPS else 2
            flips[step] = [r for r in waiting[:count] if r <= step - 1]
            waiting = waiting[len(flips[step]) :]

        def rounds_flipped_in(step):
            return flips.get(step, [])

        def e_transposes(r):
            bank = psum.tile([P, KEY_PASSES, 2, P], F32, tag="bank")
            e_bank[r] = bank
            words = e_rows[r][:].bitcast(F32).rearrange("p (g u k) -> p g u k", g=KEY_PASSES, u=2)
            return [(bank[:, g, u, :], words[:, g, u, :], ident_words[:]) for g in range(KEY_PASSES) for u in range(2)]

        def group_e(r):
            grouped = pairs.tile([P, KEY_PASSES, P, PACK], BF16, align_bytes=64)
            e_grouped[r] = grouped
            nc.scalar.copy(
                out=grouped[:].bitcast(F32),
                in_=e_bank[r][:].rearrange("p g u r -> p g r u"),
            )

        def quantise_e(r):
            codes = pairs.tile([P, KEY_PASSES, P], U32, align_bytes=64)
            scales = pairs.tile([P, KEY_PASSES, P], U8, align_bytes=64)
            e_codes[r], e_scales[r] = codes, scales
            nc.vector.quantize_mx(
                out=codes[:].rearrange("p g r -> p (g r)").bitcast(FP8X4),
                scales=scales[:].rearrange("p g r -> p (g r)"),
                in_=e_grouped[r][:].rearrange("p g r t -> p (g r t)"),
            )

        def pieces(r):
            return LAST_PIECES if r == ROUNDS - 1 else 1

        def attend(r):
            width = WIDTH // pieces(r)
            for n in range(pieces(r)):
                channels = slice(n * width, (n + 1) * width)
                bank = psum.tile([P, width], F32, tag="bank")
                o_bank[r, n] = bank
                for g in range(KEY_PASSES):
                    nc.tensor.matmul_mx(
                        out=bank[:],
                        lhsT=e_codes[r][:, g, :].bitcast(FP8X4),
                        lhsT_scale=e_scales[r][:, g, :],
                        rhs=v_codes[:, g, channels].bitcast(FP8X4),
                        rhs_scale=v_scales[:, g, channels],
                        start=(g == 0),
                        stop=(g == KEY_PASSES - 1),
                    )

        def normalise_and_store(r):
            j, qt = divmod(r, ROW_TILES)
            width = WIDTH // pieces(r)
            for n in range(pieces(r)):
                channels = slice(n * width, (n + 1) * width)
                o_rows = outs.tile([P, width], F32)
                if r in NORM_S or n == 1:
                    nc.scalar.activation(out=o_rows[:], in_=o_bank[r, n][:], func=ACT.Copy, scale=row_scale[:, r : r + 1])
                else:
                    nc.vector.tensor_scalar(
                        out=o_rows[:], in0=o_bank[r, n][:], scalar1=row_scale[:, r : r + 1], scalar2=None, op0=ALU.mult
                    )
                nc.sync.dma_start(out=out_views[j][:, qt, channels], in_=o_rows[:])

        def open_side_banks(banks):
            opened, jobs = [], []
            for words, pair, target, order in banks:
                bank, bank_jobs = word_transposes(words, pair)
                jobs += bank_jobs
                opened.append((bank, pair, target, order))
            return opened, jobs

        warm_bank = psum.tile([P, WIDTH], F32, tag="bank")

        def keep_warm(count, width):
            for n in range(count):
                nc.tensor.matmul(
                    out=warm_bank[:, :width], lhsT=zeros[:, :P], rhs=zeros[:, :width], start=True, stop=True
                )

        keep_warm(4, WIDTH)
        flip_q(nc.vector.tensor_copy, 0)
        keep_warm(2, 256)
        flip_k1(nc.scalar.copy, 0)
        keep_warm(2, 256)
        flip_k1(nc.vector.tensor_copy, 1)
        keep_warm(2, 256)
        score_pair(0, 0)
        flip_k1(nc.scalar.copy, 2)
        score_pair(0, 1)
        half_maximum(0, 0)
        flip_k1(nc.scalar.copy, 3)
        open_score_bank(0, 1)
        q_bank, q_jobs = word_transposes(q_rows[:].bitcast(F32), 1)
        score_half(1, 0)
        score_half(0, 1)
        half_maximum(1, 0)
        half_maximum(0, 1)
        negate_maximum(0)
        for job in q_jobs:
            nc.tensor.transpose(*job)
        nc.scalar.copy(out=query_slot(1), in_=q_bank[:].rearrange("p k u r -> p u k r"))
        exponentials(0)
        opened, jobs = open_side_banks(side_w(0) + side_w(1))
        for n in range(4):
            score_matmul(1, 4 + n)
            for job in jobs[4 * n : 4 * n + 4]:
                nc.tensor.transpose(*job)
        to_quantise = []
        for number, (bank, pair, target, order) in enumerate(opened):
            copy = nc.vector.tensor_copy if number % 2 == 0 else nc.scalar.copy
            to_quantise.append((empty_side_bank(copy, bank, pair, target, order), pair, target))
        half_maximum(1, 1)
        negate_maximum(1)

        to_bias = []
        for i in range(2, LAST_STEP):
            for number, v_bank in to_bias:
                add_bias(number, v_bank)
                if (number + 1) % (WIDTH // P) == 0:
                    quantise_v(number // (WIDTH // P))
            for grouped, pair, target in to_quantise:
                quantise_side_bank(grouped, pair, target)
            for r in rounds_flipped_in(i - 1):
                quantise_e(r)
            for r in rounds_flipped_in(i - 2):
                normalise_and_store(r)

            exponentials(i - 1)

            jobs = []
            for r in rounds_flipped_in(i):
                jobs += e_transposes(r)
            opened, side_jobs = open_side_banks(side_plan.get(i, []))
            scores_and_transposes(i, jobs + side_jobs)

            row_maximum(i)
            if i in RECIPS:
                reciprocal_of_row_sums(*RECIPS[i])

            for r in rounds_flipped_in(i):
                group_e(r)
            to_quantise = []
            for bank, pair, target, order in opened:
                grouped = empty_side_bank(nc.scalar.copy, bank, pair, target, order)
                if order is None:
                    to_quantise.append((grouped, pair, target))

            for r in rounds_flipped_in(i - 1):
                attend(r)
            to_bias = []
            first_bank = V_BANKS_PER_STEP * (i - FIRST_PROJECT_STEP)
            if 0 <= first_bank < V_BANKS:
                for number in range(first_bank, first_bank + V_BANKS_PER_STEP):
                    to_bias.append((number, project(number)))
